import numpy as np
import ml_dtypes


def mxq(x, axis, fmt="e4m3"):
    dtype, down = {"e4m3": (ml_dtypes.float8_e4m3fn, 7), "e5m2": (ml_dtypes.float8_e5m2, 14)}[fmt]
    v = np.moveaxis(np.asarray(x, np.float32).astype(ml_dtypes.bfloat16).astype(np.float64), axis, -1)
    blocks = v.reshape(v.shape[:-1] + (-1, 32))
    amax = np.abs(blocks).max(-1, keepdims=True)
    byte = np.maximum(np.where(amax > 0, np.frexp(amax)[1] - 1 + 127, 0) - down, 1)
    scale = np.exp2(byte - 127.0)
    codes = (blocks / scale).astype(np.float32).astype(dtype).astype(np.float64)
    return np.moveaxis((codes * scale).reshape(v.shape), -1, axis)


WIDE = False


def mx_kscale(k):
    if not WIDE:
        return np.ones(k)
    levels = np.array([30, -30])
    if k % 512:
        return np.exp2(np.random.permutation(np.resize(levels, k // 32))).repeat(32)
    a = np.empty((k // 512, 16))
    for p in range(k // 512):
        a[p, :8] = np.random.permutation(np.resize(levels, 8))
        for g in range(8):
            far = levels[np.abs(levels - a[p, g]) >= 10]
            a[p, g + 8] = far[np.random.randint(len(far))]
    return np.exp2(a.ravel()).repeat(32)


BF16 = ml_dtypes.bfloat16


def bf(x):
    return np.asarray(x, np.float32).astype(BF16)


def f64(x):
    return np.asarray(x).astype(np.float64)


E2M1 = np.array([0.0, 0.5, 1.0, 1.5, 2.0, 3.0, 4.0, 6.0, -0.0, -0.5, -1.0, -1.5, -2.0, -3.0, -4.0, -6.0])


def pack_weight(w, fmt):
    k, n = w.shape
    w = f64(bf(w)).reshape(k // 32, 32, n)
    amax = np.abs(w).max(1)
    if fmt == "e4m3":
        byte = np.frexp(amax)[1] - 1 + 127 - 7
    else:
        mant, ex = np.frexp(amax / 6.0)
        byte = np.where(mant > 0.5, ex, ex - 1) + 127
    byte = np.clip(np.where(amax > 0, byte, 1), 1, 254)
    scaled = (w * np.exp2(127.0 - byte)[:, None, :]).reshape(k, n).astype(np.float32)
    by_word = np.ascontiguousarray(scaled.reshape(k // 512, 128, 4, n).transpose(0, 1, 3, 2))
    if fmt == "e4m3":
        words = by_word.astype(ml_dtypes.float8_e4m3fn).view(np.uint8)
    else:
        c = by_word.astype(ml_dtypes.float4_e2m1fn).view(np.uint8) & 0xF
        words = c[..., 0::2] | (c[..., 1::2] << 4)
    return np.ascontiguousarray(words), np.ascontiguousarray(byte.astype(np.uint8).reshape(k // 512, 16, n))


def unpack_weight(words, scales, fmt):
    g, p, n, _ = words.shape
    if fmt == "e4m3":
        vals = np.ascontiguousarray(words).view(ml_dtypes.float8_e4m3fn).astype(np.float64)
    else:
        nib = np.empty((g, p, n, 4), np.uint8)
        nib[..., 0::2] = words & 0xF
        nib[..., 1::2] = words >> 4
        vals = E2M1[nib]
    vals = vals * np.repeat(np.exp2(scales.astype(np.float64) - 127.0), 8, axis=1)[..., None]
    return vals.transpose(0, 1, 3, 2).reshape(g * 512, n)

def pack4(w):
    words, scales = pack_weight(w, "e2m1")
    return words.reshape(words.shape[0], 128, -1), scales


def unpack4(words, scales):
    return unpack_weight(words.reshape(words.shape[0], 128, -1, 2), scales, "e2m1")


B, T, D, NH, NG = 4, 512, 1024, 8, 4
GH = (D // NH) * NG
JIT = 0.06


def angles(t, d):
    i = np.arange(d // 2, dtype=np.float64)
    theta = (10000.0 ** (-(2.0 * (i - 1.0)))) / d
    return np.arange(t, dtype=np.float64)[:, None] * theta[None, :]


def rope(y, cos, sin):
    ye, yo = y[..., 0::2], y[..., 1::2]
    oe = ye * cos + yo * sin
    oo = -ye * sin + yo * cos
    return np.stack([oe, oo], axis=-1).reshape(y.shape)


def setup_inputs():
    s = mx_kscale(D)
    aq = angles(T, D) + JIT * np.random.standard_normal((T, D // 2))
    ak = angles(T, GH) + JIT * np.random.standard_normal((T, GH // 2))
    x = bf(np.random.standard_normal((B, T, D)) * s)
    Wq_words, Wq_scales = pack4(np.random.standard_normal((D, D)) / np.sqrt(D) / s[:, None])
    Wk_words, Wk_scales = pack4(np.random.standard_normal((D, GH)) / np.sqrt(D) / s[:, None])
    Wv_words, Wv_scales = pack4(np.random.standard_normal((D, GH)) / np.sqrt(D) / s[:, None])
    return {"x": x,
            "Wq_words": Wq_words, "Wq_scales": Wq_scales,
            "Wk_words": Wk_words, "Wk_scales": Wk_scales,
            "Wv_words": Wv_words, "Wv_scales": Wv_scales,
            "cos_q": bf(np.cos(aq)), "sin_q": bf(np.sin(aq)),
            "cos_k": bf(np.cos(ak)), "sin_k": bf(np.sin(ak))}


def reference(x, Wq_words, Wq_scales, Wk_words, Wk_scales, Wv_words, Wv_scales, cos_q, sin_q, cos_k, sin_k):
    xq = mxq(f64(x), 2, "e5m2")
    q = rope(xq @ unpack4(Wq_words, Wq_scales), f64(cos_q), f64(sin_q))
    k = rope(xq @ unpack4(Wk_words, Wk_scales), f64(cos_k), f64(sin_k))
    v = xq @ unpack4(Wv_words, Wv_scales)
    return q, k, v

@@ -1,0 +1,173 @@
+from contextlib import ExitStack
+
+import concourse.mybir as mybir
+from concourse.masks import make_identity
+
+F32 = mybir.dt.float32
+BF16 = mybir.dt.bfloat16
+U8 = mybir.dt.uint8
+U32 = mybir.dt.uint32
+I32 = mybir.dt.int32
+E5M2X4 = mybir.dt.float8_e5m2_x4
+E2M1X4 = mybir.dt.float4_e2m1fn_x4
+MULT = mybir.AluOpType.mult
+ADD = mybir.AluOpType.add
+
+B, T, D = 4, 512, 1024
+NQ, NK = 1024, 512
+P = 128
+G = D // 512
+TT = T // P
+NTILES = B * TT
+FLOPS = 2 * B * T * D * (NQ + 2 * NK)
+
+GROUPS = [[0], [1]] + [[n, n + 1] for n in range(2, NTILES, 2)]
+
+
+def tile_selfattn_pa_kernel(tc, x, wq_words, wq_scales, wk_words, wk_scales, wv_words, wv_scales,
+                                        cos_q, sin_q, cos_k, sin_k, out_q, out_k, out_v):
+    nc = tc.nc
+    with ExitStack() as ctx:
+        keep = ctx.enter_context(tc.tile_pool(name="keep", bufs=1))
+        work = ctx.enter_context(tc.tile_pool(name="work", bufs=3))
+        psum = ctx.enter_context(tc.psum_pool(name="psum", bufs=2))
+        ctx.enter_context(tc.manual_schedule())
+
+        planes = {}
+        words = {}
+        for key, width in (("q", NQ), ("k", NK), ("v", NK)):
+            planes[key] = keep.tile([P, G, width], U8, name="plane_" + key, align_bytes=64)
+            words[key] = keep.tile([P, G, 2 * width], U8, name="words_" + key, align_bytes=64)
+            nc.vector.memset(planes[key][:].rearrange("p g n -> p (g n)").bitcast(I32), 0)
+        warm = keep.tile([P, 2], F32, name="warm")
+        nc.vector.memset(warm[:, 0:1], 0.0)
+        nc.scalar.copy(out=warm[:, 1:2], in_=warm[:, 0:1])
+        ident = keep.tile([P, P], F32, name="ident")
+        make_identity(nc, ident[:])
+
+        x_sb = []
+        for gi, tiles in enumerate(GROUPS):
+            x_sb.append(keep.tile([P, len(tiles), D], BF16, name="x%d" % gi))
+        tab_q = [keep.tile([P, 2, 2, NQ // 2], BF16, name="tabq%d" % tt) for tt in range(TT)]
+        tab_k = [keep.tile([P, 2, 2, NK // 2], BF16, name="tabk%d" % tt) for tt in range(TT)]
+
+        def load_x(gi):
+            tiles = GROUPS[gi]
+            tt, b0 = divmod(tiles[0], B)
+            nc.sync.dma_start(out=x_sb[gi][:],
+                              in_=x[b0:b0 + len(tiles), tt * P:(tt + 1) * P, :].rearrange("b p k -> p b k"))
+
+        def load_weight(key, w_words, w_scales):
+            for quad in range(4):
+                nc.sync.dma_start(
+                    out=planes[key][32 * quad:32 * quad + 4, :, :].bitcast(I32),
+                    in_=w_scales[:, 4 * quad:4 * quad + 4, :].rearrange("g r n -> r g n").bitcast(I32))
+            nc.sync.dma_start(out=words[key][:].bitcast(I32), in_=w_words.rearrange("g p n -> p g n").bitcast(I32))
+
+        def load_table(tab, cos, sin, tt):
+            nc.sync.dma_start(out=tab[tt][:, 0, 0, :], in_=cos[tt * P:(tt + 1) * P, :])
+            nc.sync.dma_start(out=tab[tt][:, 1, 1, :], in_=sin[tt * P:(tt + 1) * P, :])
+
+        def prep_table(tab, tt):
+            nc.scalar.copy(out=tab[tt][:, 0, 1, :], in_=tab[tt][:, 0, 0, :])
+            nc.scalar.mul(out=tab[tt][:, 1, 0, :], in_=tab[tt][:, 1, 1, :], mul=-1.0)
+
+        load_x(0)
+        load_x(1)
+        load_weight("q", wq_words, wq_scales)
+        load_table(tab_q, cos_q, sin_q, 0)
+        load_weight("k", wk_words, wk_scales)
+        load_table(tab_k, cos_k, sin_k, 0)
+        load_weight("v", wv_words, wv_scales)
+        load_x(2)
+        for tt in range(1, TT):
+            load_table(tab_q, cos_q, sin_q, tt)
+            load_table(tab_k, cos_k, sin_k, tt)
+            load_x(2 * tt + 1)
+            load_x(2 * tt + 2)
+
+        codes_of = {}
+
+        def prep_group(gi):
+            tiles = GROUPS[gi]
+            n = len(tiles)
+            grouped = work.tile([P, n * 1024], BF16, name="grouped", tag="grouped", align_bytes=64)
+            for a in range(n):
+                xw = x_sb[gi][:, a, :].bitcast(F32)
+                xt = psum.tile([P, 512], F32, name="xt", tag="xt", bufs=2)
+                for g in range(G):
+                    for u in range(2):
+                        s = 2 * g + u
+                        nc.tensor.transpose(xt[:, s * P:(s + 1) * P], xw[:, 256 * g + u:256 * (g + 1):2], ident[:])
+                nc.scalar.copy(
+                    out=grouped[:, a * 1024:(a + 1) * 1024].bitcast(F32).rearrange("p (g r u) -> p g r u", g=G, u=2),
+                    in_=xt[:].rearrange("p (g u r) -> p g r u", g=G, u=2))
+            codes = work.tile([P, n * 256], U32, name="codes", tag="codes", align_bytes=64)
+            xs = work.tile([P, n * 256], U8, name="xs", tag="xs", align_bytes=64)
+            nc.vector.quantize_mx(out=codes[:].bitcast(E5M2X4), scales=xs[:], in_=grouped[:])
+            for a, t in enumerate(tiles):
+                codes_of[t] = (codes, xs, a)
+
+        def project(t, key, j):
+            codes, xs, a = codes_of[t]
+            acc = psum.tile([P, 512], F32, name="acc", tag="acc", bufs=6)
+            for g in range(G):
+                cols = slice(a * 256 + g * P, a * 256 + (g + 1) * P)
+                nc.tensor.matmul_mx(out=acc[:], lhsT=codes[:, cols].bitcast(E5M2X4), lhsT_scale=xs[:, cols],
+                                    rhs=words[key][:, g, 1024 * j:1024 * (j + 1)].bitcast(E2M1X4),
+                                    rhs_scale=planes[key][:, g, 512 * j:512 * (j + 1)],
+                                    start=(g == 0), stop=(g == G - 1))
+            return acc
+
+        def products(acc, at, tab, j):
+            nc.vector.tensor_tensor(
+                out=at[:, :, 512 * j:512 * (j + 1)].rearrange("p w (i e) -> p w i e", e=2),
+                in0=acc[:].rearrange("p (i e) -> p i e", e=2).unsqueeze(1).to_broadcast([P, 2, 256, 2]),
+                in1=tab[:, :, :, 256 * j:256 * (j + 1)].rearrange("p w e i -> p w i e"),
+                op=MULT)
+
+        def combine(at, res):
+            nc.gpsimd.tensor_tensor(
+                out=res[:].rearrange("p (i e) -> p i e", e=2),
+                in0=at[:, 0, :].rearrange("p (i e) -> p i e", e=2),
+                in1=at[:, 1, :].rearrange("p (i e) -> p i e", e=2)[:, :, ::-1],
+                op=ADD)
+
+        first_of = {}
+        for gi, tiles in enumerate(GROUPS):
+            first_of[tiles[0]] = gi
+
+        prep_group(0)
+        prep_group(1)
+        prep_table(tab_q, 0)
+        prep_table(tab_k, 0)
+
+        for t in range(NTILES):
+            tt, b = divmod(t, B)
+            rows = slice(tt * P, (tt + 1) * P)
+
+            at_q = work.tile([P, 2, NQ], F32, name="at_q", tag="at_q")
+            for j in range(2):
+                acc = project(t, "q", j)
+                products(acc, at_q, tab_q[tt], j)
+            res_q = work.tile([P, NQ], F32, name="res_q", tag="res_q")
+            combine(at_q, res_q)
+            nc.sync.dma_start(out=out_q[b, rows, :], in_=res_q[:])
+
+            at_k = work.tile([P, 2, NK], F32, name="at_k", tag="at_k")
+            acc = project(t, "k", 0)
+            products(acc, at_k, tab_k[tt], 0)
+            res_k = work.tile([P, NK], F32, name="res_k", tag="res_k")
+            combine(at_k, res_k)
+            nc.sync.dma_start(out=out_k[b, rows, :], in_=res_k[:])
+
+            acc = project(t, "v", 0)
+            res_v = work.tile([P, NK], F32, name="res_v", tag="res_v")
+            nc.scalar.copy(out=res_v[:], in_=acc[:])
+            nc.sync.dma_start(out=out_v[b, rows, :], in_=res_v[:])
+
+            if t + 2 in first_of:
+                prep_group(first_of[t + 2])
+            if b == 1 and tt + 1 < TT:
+                prep_table(tab_q, tt + 1)
+                prep_table(tab_k, tt + 1)

@@ -21,7 +21,9 @@ TT = T // P
 NTILES = B * TT
 FLOPS = 2 * B * T * D * (NQ + 2 * NK)
 
-GROUPS = [[0], [1]] + [[n, n + 1] for n in range(2, NTILES, 2)]
+XLOADS = [[0], [1]] + [[n, n + 1] for n in range(2, NTILES, 2)]
+QGROUPS = [[0], [1], [2, 3], [4, 5, 6, 7], [8, 9, 10, 11], [12, 13, 14, 15]]
+NR = NQ + NK
 
 
 def tile_selfattn_pa_kernel(tc, x, wq_words, wq_scales, wk_words, wk_scales, wv_words, wv_scales,
@@ -45,16 +47,19 @@ def tile_selfattn_pa_kernel(tc, x, wq_words, wq_scales, wk_words, wk_scales, wv_
         ident = keep.tile([P, P], F32, name="ident")
         make_identity(nc, ident[:])
 
+        x_of = {}
         x_sb = []
-        for gi, tiles in enumerate(GROUPS):
-            x_sb.append(keep.tile([P, len(tiles), D], BF16, name="x%d" % gi))
+        for li, tiles in enumerate(XLOADS):
+            x_sb.append(keep.tile([P, len(tiles), D], BF16, name="x%d" % li))
+            for a, t in enumerate(tiles):
+                x_of[t] = (li, a)
         tab_q = [keep.tile([P, 2, 2, NQ // 2], BF16, name="tabq%d" % tt) for tt in range(TT)]
         tab_k = [keep.tile([P, 2, 2, NK // 2], BF16, name="tabk%d" % tt) for tt in range(TT)]
 
-        def load_x(gi):
-            tiles = GROUPS[gi]
+        def load_x(li):
+            tiles = XLOADS[li]
             tt, b0 = divmod(tiles[0], B)
-            nc.sync.dma_start(out=x_sb[gi][:],
+            nc.sync.dma_start(out=x_sb[li][:],
                               in_=x[b0:b0 + len(tiles), tt * P:(tt + 1) * P, :].rearrange("b p k -> p b k"))
 
         def load_weight(key, w_words, w_scales):
@@ -66,50 +71,59 @@ def tile_selfattn_pa_kernel(tc, x, wq_words, wq_scales, wk_words, wk_scales, wv_
 
         def load_table(tab, cos, sin, tt):
             nc.sync.dma_start(out=tab[tt][:, 0, 0, :], in_=cos[tt * P:(tt + 1) * P, :])
-            nc.sync.dma_start(out=tab[tt][:, 1, 1, :], in_=sin[tt * P:(tt + 1) * P, :])
+            nc.sync.dma_start(out=tab[tt][:, 1, 0, :], in_=sin[tt * P:(tt + 1) * P, :])
 
         def prep_table(tab, tt):
-            nc.scalar.copy(out=tab[tt][:, 0, 1, :], in_=tab[tt][:, 0, 0, :])
-            nc.scalar.mul(out=tab[tt][:, 1, 0, :], in_=tab[tt][:, 1, 1, :], mul=-1.0)
+            nc.scalar.copy(out=tab[tt][:, 1, 1, :], in_=tab[tt][:, 0, 0, :])
+            nc.scalar.mul(out=tab[tt][:, 0, 1, :], in_=tab[tt][:, 1, 0, :], mul=-1.0)
 
         load_x(0)
         load_x(1)
         load_weight("q", wq_words, wq_scales)
         load_table(tab_q, cos_q, sin_q, 0)
+        load_x(2)
         load_weight("k", wk_words, wk_scales)
         load_table(tab_k, cos_k, sin_k, 0)
         load_weight("v", wv_words, wv_scales)
-        load_x(2)
         for tt in range(1, TT):
-            load_table(tab_q, cos_q, sin_q, tt)
-            load_table(tab_k, cos_k, sin_k, tt)
             load_x(2 * tt + 1)
             load_x(2 * tt + 2)
+            load_table(tab_q, cos_q, sin_q, tt)
+            load_table(tab_k, cos_k, sin_k, tt)
 
+        group_of = {}
+        for qi, tiles in enumerate(QGROUPS):
+            for a, t in enumerate(tiles):
+                group_of[t] = (qi, a)
+        grouped_of = {}
         codes_of = {}
 
-        def prep_group(gi):
-            tiles = GROUPS[gi]
-            n = len(tiles)
-            grouped = work.tile([P, n * 1024], BF16, name="grouped", tag="grouped", align_bytes=64)
-            for a in range(n):
-                xw = x_sb[gi][:, a, :].bitcast(F32)
-                xt = psum.tile([P, 512], F32, name="xt", tag="xt", bufs=2)
-                for g in range(G):
-                    for u in range(2):
-                        s = 2 * g + u
-                        nc.tensor.transpose(xt[:, s * P:(s + 1) * P], xw[:, 256 * g + u:256 * (g + 1):2], ident[:])
-                nc.scalar.copy(
-                    out=grouped[:, a * 1024:(a + 1) * 1024].bitcast(F32).rearrange("p (g r u) -> p g r u", g=G, u=2),
-                    in_=xt[:].rearrange("p (g u r) -> p g r u", g=G, u=2))
+        def turn(t):
+            qi, a = group_of[t]
+            if a == 0:
+                grouped_of[qi] = work.tile([P, len(QGROUPS[qi]) * 1024], BF16, name="grouped", tag="grouped",
+                                           bufs=2, align_bytes=64)
+            li, xa = x_of[t]
+            xw = x_sb[li][:, xa, :].bitcast(F32)
+            xt = psum.tile([P, 512], F32, name="xt", tag="xt", bufs=2)
+            for g in range(G):
+                for u in range(2):
+                    s = 2 * g + u
+                    nc.tensor.transpose(xt[:, s * P:(s + 1) * P], xw[:, 256 * g + u:256 * (g + 1):2], ident[:])
+            nc.scalar.copy(
+                out=grouped_of[qi][:, a * 1024:(a + 1) * 1024].bitcast(F32).rearrange("p (g r u) -> p g r u", g=G, u=2),
+                in_=xt[:].rearrange("p (g u r) -> p g r u", g=G, u=2))
+
+        def quantize(qi):
+            n = len(QGROUPS[qi])
             codes = work.tile([P, n * 256], U32, name="codes", tag="codes", align_bytes=64)
             xs = work.tile([P, n * 256], U8, name="xs", tag="xs", align_bytes=64)
-            nc.vector.quantize_mx(out=codes[:].bitcast(E5M2X4), scales=xs[:], in_=grouped[:])
-            for a, t in enumerate(tiles):
-                codes_of[t] = (codes, xs, a)
+            nc.vector.quantize_mx(out=codes[:].bitcast(E5M2X4), scales=xs[:], in_=grouped_of[qi][:])
+            codes_of[qi] = (codes, xs)
 
         def project(t, key, j):
-            codes, xs, a = codes_of[t]
+            qi, a = group_of[t]
+            codes, xs = codes_of[qi]
             acc = psum.tile([P, 512], F32, name="acc", tag="acc", bufs=6)
             for g in range(G):
                 cols = slice(a * 256 + g * P, a * 256 + (g + 1) * P)
@@ -119,55 +133,60 @@ def tile_selfattn_pa_kernel(tc, x, wq_words, wq_scales, wk_words, wk_scales, wv_
                                     start=(g == 0), stop=(g == G - 1))
             return acc
 
-        def products(acc, at, tab, j):
+        def products(acc, at, off, tab, j):
             nc.vector.tensor_tensor(
-                out=at[:, :, 512 * j:512 * (j + 1)].rearrange("p w (i e) -> p w i e", e=2),
-                in0=acc[:].rearrange("p (i e) -> p i e", e=2).unsqueeze(1).to_broadcast([P, 2, 256, 2]),
+                out=at[:, :, off:off + 512].rearrange("p w (i e) -> p w i e", e=2),
+                in0=acc[:].rearrange("p (i w) -> p w i", w=2).unsqueeze(3).to_broadcast([P, 2, 256, 2]),
                 in1=tab[:, :, :, 256 * j:256 * (j + 1)].rearrange("p w e i -> p w i e"),
                 op=MULT)
 
-        def combine(at, res):
-            nc.gpsimd.tensor_tensor(
-                out=res[:].rearrange("p (i e) -> p i e", e=2),
-                in0=at[:, 0, :].rearrange("p (i e) -> p i e", e=2),
-                in1=at[:, 1, :].rearrange("p (i e) -> p i e", e=2)[:, :, ::-1],
-                op=ADD)
-
-        first_of = {}
-        for gi, tiles in enumerate(GROUPS):
-            first_of[tiles[0]] = gi
-
-        prep_group(0)
-        prep_group(1)
+        turn(0)
+        quantize(0)
+        turn(1)
+        quantize(1)
         prep_table(tab_q, 0)
         prep_table(tab_k, 0)
 
         for t in range(NTILES):
             tt, b = divmod(t, B)
             rows = slice(tt * P, (tt + 1) * P)
+            last = t == NTILES - 1
 
-            at_q = work.tile([P, 2, NQ], F32, name="at_q", tag="at_q")
+            at = work.tile([P, 2, NR], F32, name="at", tag="at")
             for j in range(2):
                 acc = project(t, "q", j)
-                products(acc, at_q, tab_q[tt], j)
-            res_q = work.tile([P, NQ], F32, name="res_q", tag="res_q")
-            combine(at_q, res_q)
-            nc.sync.dma_start(out=out_q[b, rows, :], in_=res_q[:])
-
-            at_k = work.tile([P, 2, NK], F32, name="at_k", tag="at_k")
+                products(acc, at, 512 * j, tab_q[tt], j)
+            if t == 0:
+                turn(2)
+                turn(3)
+                quantize(2)
             acc = project(t, "k", 0)
-            products(acc, at_k, tab_k[tt], 0)
-            res_k = work.tile([P, NK], F32, name="res_k", tag="res_k")
-            combine(at_k, res_k)
-            nc.sync.dma_start(out=out_k[b, rows, :], in_=res_k[:])
+            products(acc, at, NQ, tab_k[tt], 0)
 
             acc = project(t, "v", 0)
             res_v = work.tile([P, NK], F32, name="res_v", tag="res_v")
             nc.scalar.copy(out=res_v[:], in_=acc[:])
-            nc.sync.dma_start(out=out_v[b, rows, :], in_=res_v[:])
+            nc.scalar.dma_start(out=out_v[b, rows, :], in_=res_v[:])
 
-            if t + 2 in first_of:
-                prep_group(first_of[t + 2])
+            res = work.tile([P, NR], F32, name="res", tag="res")
+            if not last:
+                nc.gpsimd.tensor_tensor(out=res[:], in0=at[:, 0, :], in1=at[:, 1, :], op=ADD)
+                nc.sync.dma_start(out=out_q[b, rows, :], in_=res[:, 0:NQ])
+                nc.sync.dma_start(out=out_k[b, rows, :], in_=res[:, NQ:NR])
+            else:
+                for j in range(3):
+                    cols = slice(512 * j, 512 * (j + 1))
+                    nc.vector.tensor_tensor(out=res[:, cols], in0=at[:, 0, cols], in1=at[:, 1, cols], op=ADD)
+                    if j < 2:
+                        nc.sync.dma_start(out=out_q[b, rows, cols], in_=res[:, cols])
+                    else:
+                        nc.sync.dma_start(out=out_k[b, rows, :], in_=res[:, cols])
+
+            if b in (0, 1) and tt + 1 < TT:
+                turn(4 * tt + 4 + 2 * b)
+                turn(4 * tt + 5 + 2 * b)
+            if b == 2 and tt + 1 < TT:
+                quantize(tt + 3)
             if b == 1 and tt + 1 < TT:
                 prep_table(tab_q, tt + 1)
                 prep_table(tab_k, tt + 1)

@@ -24,6 +24,7 @@ FLOPS = 2 * B * T * D * (NQ + 2 * NK)
 XLOADS = [[0], [1]] + [[n, n + 1] for n in range(2, NTILES, 2)]
 QGROUPS = [[0], [1], [2, 3], [4, 5, 6, 7], [8, 9, 10, 11], [12, 13, 14, 15]]
 NR = NQ + NK
+WARM = 5
 
 
 def tile_selfattn_pa_kernel(tc, x, wq_words, wq_scales, wk_words, wk_scales, wv_words, wv_scales,
@@ -34,6 +35,12 @@ def tile_selfattn_pa_kernel(tc, x, wq_words, wq_scales, wk_words, wk_scales, wv_
         work = ctx.enter_context(tc.tile_pool(name="work", bufs=3))
         psum = ctx.enter_context(tc.psum_pool(name="psum", bufs=2))
         ctx.enter_context(tc.manual_schedule())
+
+        zeros = keep.tile([P, 512], BF16, name="zeros")
+        nc.gpsimd.memset(zeros[:], 0.0)
+        idle = psum.tile([P, 512], F32, name="acc", tag="acc", bufs=6)
+        for i in range(WARM):
+            nc.tensor.matmul(out=idle[:], lhsT=zeros[:, 0:P], rhs=zeros[:], start=True, stop=True)
 
         planes = {}
         words = {}
@@ -56,10 +63,10 @@ def tile_selfattn_pa_kernel(tc, x, wq_words, wq_scales, wk_words, wk_scales, wv_
         tab_q = [keep.tile([P, 2, 2, NQ // 2], BF16, name="tabq%d" % tt) for tt in range(TT)]
         tab_k = [keep.tile([P, 2, 2, NK // 2], BF16, name="tabk%d" % tt) for tt in range(TT)]
 
-        def load_x(li):
+        def load_x(li, queue):
             tiles = XLOADS[li]
             tt, b0 = divmod(tiles[0], B)
-            nc.sync.dma_start(out=x_sb[li][:],
+            queue.dma_start(out=x_sb[li][:],
                               in_=x[b0:b0 + len(tiles), tt * P:(tt + 1) * P, :].rearrange("b p k -> p b k"))
 
         def load_weight(key, w_words, w_scales):
@@ -77,17 +84,17 @@ def tile_selfattn_pa_kernel(tc, x, wq_words, wq_scales, wk_words, wk_scales, wv_
             nc.scalar.copy(out=tab[tt][:, 1, 1, :], in_=tab[tt][:, 0, 0, :])
             nc.scalar.mul(out=tab[tt][:, 0, 1, :], in_=tab[tt][:, 1, 0, :], mul=-1.0)
 
-        load_x(0)
-        load_x(1)
+        load_x(0, nc.sync)
+        load_x(1, nc.sync)
+        load_x(2, nc.gpsimd)
         load_weight("q", wq_words, wq_scales)
         load_table(tab_q, cos_q, sin_q, 0)
-        load_x(2)
         load_weight("k", wk_words, wk_scales)
         load_table(tab_k, cos_k, sin_k, 0)
         load_weight("v", wv_words, wv_scales)
         for tt in range(1, TT):
-            load_x(2 * tt + 1)
-            load_x(2 * tt + 2)
+            load_x(2 * tt + 1, nc.sync)
+            load_x(2 * tt + 2, nc.sync)
             load_table(tab_q, cos_q, sin_q, tt)
             load_table(tab_k, cos_k, sin_k, tt)
 
@@ -133,43 +140,44 @@ def tile_selfattn_pa_kernel(tc, x, wq_words, wq_scales, wk_words, wk_scales, wv_
                                     start=(g == 0), stop=(g == G - 1))
             return acc
 
-        def products(acc, at, off, tab, j):
-            nc.vector.tensor_tensor(
+        def products(engine, acc, at, off, tab, j):
+            engine.tensor_tensor(
                 out=at[:, :, off:off + 512].rearrange("p w (i e) -> p w i e", e=2),
                 in0=acc[:].rearrange("p (i w) -> p w i", w=2).unsqueeze(3).to_broadcast([P, 2, 256, 2]),
                 in1=tab[:, :, :, 256 * j:256 * (j + 1)].rearrange("p w e i -> p w i e"),
                 op=MULT)
 
-        turn(0)
-        quantize(0)
-        turn(1)
-        quantize(1)
-        prep_table(tab_q, 0)
-        prep_table(tab_k, 0)
+        at_of = {}
 
-        for t in range(NTILES):
+        def bank(t, key, j, on_gpsimd=False):
+            tt = t // B
+            if t not in at_of:
+                at_of[t] = work.tile([P, 2, NR], F32, name="at", tag="at", bufs=4)
+            y = project(t, key, j)
+            engine = nc.vector
+            if on_gpsimd:
+                y_sb = work.tile([P, 512], F32, name="y_sb", tag="y_sb", bufs=1)
+                nc.scalar.copy(out=y_sb[:], in_=y[:])
+                y = y_sb
+                engine = nc.gpsimd
+            if key == "q":
+                products(engine, y, at_of[t], 512 * j, tab_q[tt], j)
+            else:
+                products(engine, y, at_of[t], NQ, tab_k[tt], 0)
+
+        def values(t):
             tt, b = divmod(t, B)
-            rows = slice(tt * P, (tt + 1) * P)
-            last = t == NTILES - 1
-
-            at = work.tile([P, 2, NR], F32, name="at", tag="at")
-            for j in range(2):
-                acc = project(t, "q", j)
-                products(acc, at, 512 * j, tab_q[tt], j)
-            if t == 0:
-                turn(2)
-                turn(3)
-                quantize(2)
-            acc = project(t, "k", 0)
-            products(acc, at, NQ, tab_k[tt], 0)
-
             acc = project(t, "v", 0)
             res_v = work.tile([P, NK], F32, name="res_v", tag="res_v")
             nc.scalar.copy(out=res_v[:], in_=acc[:])
-            nc.scalar.dma_start(out=out_v[b, rows, :], in_=res_v[:])
+            nc.scalar.dma_start(out=out_v[b, tt * P:(tt + 1) * P, :], in_=res_v[:])
 
+        def combine(t):
+            tt, b = divmod(t, B)
+            rows = slice(tt * P, (tt + 1) * P)
+            at = at_of[t]
             res = work.tile([P, NR], F32, name="res", tag="res")
-            if not last:
+            if t < NTILES - 1:
                 nc.gpsimd.tensor_tensor(out=res[:], in0=at[:, 0, :], in1=at[:, 1, :], op=ADD)
                 nc.sync.dma_start(out=out_q[b, rows, :], in_=res[:, 0:NQ])
                 nc.sync.dma_start(out=out_k[b, rows, :], in_=res[:, NQ:NR])
@@ -182,11 +190,41 @@ def tile_selfattn_pa_kernel(tc, x, wq_words, wq_scales, wk_words, wk_scales, wv_
                     else:
                         nc.sync.dma_start(out=out_k[b, rows, :], in_=res[:, cols])
 
-            if b in (0, 1) and tt + 1 < TT:
-                turn(4 * tt + 4 + 2 * b)
-                turn(4 * tt + 5 + 2 * b)
-            if b == 2 and tt + 1 < TT:
+        def look_ahead(t):
+            tt, b = divmod(t, B)
+            if tt + 1 < TT and b in (1, 2):
+                turn(4 * tt + 2 + 2 * b)
+                turn(4 * tt + 3 + 2 * b)
+            if tt + 1 < TT and b == 2:
                 quantize(tt + 3)
-            if b == 1 and tt + 1 < TT:
+            if tt + 1 < TT and b == 1:
                 prep_table(tab_q, tt + 1)
                 prep_table(tab_k, tt + 1)
+
+        turn(0)
+        quantize(0)
+        turn(1)
+        quantize(1)
+        prep_table(tab_q, 0)
+        bank(0, "q", 0)
+        bank(0, "q", 1, on_gpsimd=True)
+        bank(1, "q", 0)
+        bank(1, "q", 1)
+        turn(2)
+        turn(3)
+        quantize(2)
+        prep_table(tab_k, 0)
+        bank(0, "k", 0)
+        combine(0)
+        bank(1, "k", 0)
+        combine(1)
+        values(0)
+        values(1)
+        look_ahead(1)
+        for t in range(2, NTILES):
+            bank(t, "q", 0)
+            bank(t, "q", 1)
+            bank(t, "k", 0)
+            values(t)
+            combine(t)
+            look_ahead(t)

@@ -24,7 +24,6 @@ FLOPS = 2 * B * T * D * (NQ + 2 * NK)
 XLOADS = [[0], [1]] + [[n, n + 1] for n in range(2, NTILES, 2)]
 QGROUPS = [[0], [1], [2, 3], [4, 5, 6, 7], [8, 9, 10, 11], [12, 13, 14, 15]]
 NR = NQ + NK
-WARM = 5
 
 
 def tile_selfattn_pa_kernel(tc, x, wq_words, wq_scales, wk_words, wk_scales, wv_words, wv_scales,
@@ -35,12 +34,6 @@ def tile_selfattn_pa_kernel(tc, x, wq_words, wq_scales, wk_words, wk_scales, wv_
         work = ctx.enter_context(tc.tile_pool(name="work", bufs=3))
         psum = ctx.enter_context(tc.psum_pool(name="psum", bufs=2))
         ctx.enter_context(tc.manual_schedule())
-
-        zeros = keep.tile([P, 512], BF16, name="zeros")
-        nc.gpsimd.memset(zeros[:], 0.0)
-        idle = psum.tile([P, 512], F32, name="acc", tag="acc", bufs=6)
-        for i in range(WARM):
-            nc.tensor.matmul(out=idle[:], lhsT=zeros[:, 0:P], rhs=zeros[:], start=True, stop=True)
 
         planes = {}
         words = {}
@@ -63,10 +56,17 @@ def tile_selfattn_pa_kernel(tc, x, wq_words, wq_scales, wk_words, wk_scales, wv_
         tab_q = [keep.tile([P, 2, 2, NQ // 2], BF16, name="tabq%d" % tt) for tt in range(TT)]
         tab_k = [keep.tile([P, 2, 2, NK // 2], BF16, name="tabk%d" % tt) for tt in range(TT)]
 
-        def load_x(li, queue):
+        tabx_q = [None] + [keep.tile([P, 2, NQ], BF16, name="tabxq%d" % tt) for tt in range(1, TT)]
+        tabx_k = [None] + [keep.tile([P, 2, NK], BF16, name="tabxk%d" % tt) for tt in range(1, TT)]
+
+        def spread_table(tab, tabx, tt, w):
+            nc.scalar.copy(out=tabx[tt][:, w, :].rearrange("p (i e) -> p i e", e=2),
+                           in_=tab[tt][:, w, :, :].rearrange("p e i -> p i e"))
+
+        def load_x(li):
             tiles = XLOADS[li]
             tt, b0 = divmod(tiles[0], B)
-            queue.dma_start(out=x_sb[li][:],
+            nc.sync.dma_start(out=x_sb[li][:],
                               in_=x[b0:b0 + len(tiles), tt * P:(tt + 1) * P, :].rearrange("b p k -> p b k"))
 
         def load_weight(key, w_words, w_scales):
@@ -84,17 +84,17 @@ def tile_selfattn_pa_kernel(tc, x, wq_words, wq_scales, wk_words, wk_scales, wv_
             nc.scalar.copy(out=tab[tt][:, 1, 1, :], in_=tab[tt][:, 0, 0, :])
             nc.scalar.mul(out=tab[tt][:, 0, 1, :], in_=tab[tt][:, 1, 0, :], mul=-1.0)
 
-        load_x(0, nc.sync)
-        load_x(1, nc.sync)
-        load_x(2, nc.gpsimd)
+        load_x(0)
+        load_x(1)
         load_weight("q", wq_words, wq_scales)
         load_table(tab_q, cos_q, sin_q, 0)
+        load_x(2)
         load_weight("k", wk_words, wk_scales)
         load_table(tab_k, cos_k, sin_k, 0)
         load_weight("v", wv_words, wv_scales)
         for tt in range(1, TT):
-            load_x(2 * tt + 1, nc.sync)
-            load_x(2 * tt + 2, nc.sync)
+            load_x(2 * tt + 1)
+            load_x(2 * tt + 2)
             load_table(tab_q, cos_q, sin_q, tt)
             load_table(tab_k, cos_k, sin_k, tt)
 
@@ -140,44 +140,47 @@ def tile_selfattn_pa_kernel(tc, x, wq_words, wq_scales, wk_words, wk_scales, wv_
                                     start=(g == 0), stop=(g == G - 1))
             return acc
 
-        def products(engine, acc, at, off, tab, j):
-            engine.tensor_tensor(
+        def products(acc, at, off, tab, tabx, j):
+            if tabx is None:
+                factors = tab[:, :, :, 256 * j:256 * (j + 1)].rearrange("p w e i -> p w i e")
+            else:
+                factors = tabx[:, :, 512 * j:512 * (j + 1)].rearrange("p w (i e) -> p w i e", e=2)
+            nc.vector.tensor_tensor(
                 out=at[:, :, off:off + 512].rearrange("p w (i e) -> p w i e", e=2),
                 in0=acc[:].rearrange("p (i w) -> p w i", w=2).unsqueeze(3).to_broadcast([P, 2, 256, 2]),
-                in1=tab[:, :, :, 256 * j:256 * (j + 1)].rearrange("p w e i -> p w i e"),
+                in1=factors,
                 op=MULT)
 
-        at_of = {}
+        turn(0)
+        quantize(0)
+        turn(1)
+        quantize(1)
+        prep_table(tab_q, 0)
+        prep_table(tab_k, 0)
 
-        def bank(t, key, j, on_gpsimd=False):
-            tt = t // B
-            if t not in at_of:
-                at_of[t] = work.tile([P, 2, NR], F32, name="at", tag="at", bufs=4)
-            y = project(t, key, j)
-            engine = nc.vector
-            if on_gpsimd:
-                y_sb = work.tile([P, 512], F32, name="y_sb", tag="y_sb", bufs=1)
-                nc.scalar.copy(out=y_sb[:], in_=y[:])
-                y = y_sb
-                engine = nc.gpsimd
-            if key == "q":
-                products(engine, y, at_of[t], 512 * j, tab_q[tt], j)
-            else:
-                products(engine, y, at_of[t], NQ, tab_k[tt], 0)
-
-        def values(t):
+        for t in range(NTILES):
             tt, b = divmod(t, B)
+            rows = slice(tt * P, (tt + 1) * P)
+            last = t == NTILES - 1
+
+            at = work.tile([P, 2, NR], F32, name="at", tag="at")
+            for j in range(2):
+                acc = project(t, "q", j)
+                products(acc, at, 512 * j, tab_q[tt], tabx_q[tt], j)
+            if t == 0:
+                turn(2)
+                turn(3)
+                quantize(2)
+            acc = project(t, "k", 0)
+            products(acc, at, NQ, tab_k[tt], tabx_k[tt], 0)
+
             acc = project(t, "v", 0)
             res_v = work.tile([P, NK], F32, name="res_v", tag="res_v")
             nc.scalar.copy(out=res_v[:], in_=acc[:])
-            nc.scalar.dma_start(out=out_v[b, tt * P:(tt + 1) * P, :], in_=res_v[:])
+            nc.scalar.dma_start(out=out_v[b, rows, :], in_=res_v[:])
 
-        def combine(t):
-            tt, b = divmod(t, B)
-            rows = slice(tt * P, (tt + 1) * P)
-            at = at_of[t]
             res = work.tile([P, NR], F32, name="res", tag="res")
-            if t < NTILES - 1:
+            if not last:
                 nc.gpsimd.tensor_tensor(out=res[:], in0=at[:, 0, :], in1=at[:, 1, :], op=ADD)
                 nc.sync.dma_start(out=out_q[b, rows, :], in_=res[:, 0:NQ])
                 nc.sync.dma_start(out=out_k[b, rows, :], in_=res[:, NQ:NR])
@@ -190,41 +193,16 @@ def tile_selfattn_pa_kernel(tc, x, wq_words, wq_scales, wk_words, wk_scales, wv_
                     else:
                         nc.sync.dma_start(out=out_k[b, rows, :], in_=res[:, cols])
 
-        def look_ahead(t):
-            tt, b = divmod(t, B)
-            if tt + 1 < TT and b in (1, 2):
-                turn(4 * tt + 2 + 2 * b)
-                turn(4 * tt + 3 + 2 * b)
-            if tt + 1 < TT and b == 2:
+            if b in (0, 1) and tt + 1 < TT:
+                turn(4 * tt + 4 + 2 * b)
+                turn(4 * tt + 5 + 2 * b)
+            if b == 2 and tt + 1 < TT:
                 quantize(tt + 3)
-            if tt + 1 < TT and b == 1:
+            if b == 1 and tt + 1 < TT:
                 prep_table(tab_q, tt + 1)
                 prep_table(tab_k, tt + 1)
-
-        turn(0)
-        quantize(0)
-        turn(1)
-        quantize(1)
-        prep_table(tab_q, 0)
-        bank(0, "q", 0)
-        bank(0, "q", 1, on_gpsimd=True)
-        bank(1, "q", 0)
-        bank(1, "q", 1)
-        turn(2)
-        turn(3)
-        quantize(2)
-        prep_table(tab_k, 0)
-        bank(0, "k", 0)
-        combine(0)
-        bank(1, "k", 0)
-        combine(1)
-        values(0)
-        values(1)
-        look_ahead(1)
-        for t in range(2, NTILES):
-            bank(t, "q", 0)
-            bank(t, "q", 1)
-            bank(t, "k", 0)
-            values(t)
-            combine(t)
-            look_ahead(t)
+                spread_table(tab_q, tabx_q, tt + 1, 0)
+            if b == 2 and tt + 1 < TT:
+                spread_table(tab_q, tabx_q, tt + 1, 1)
+                spread_table(tab_k, tabx_k, tt + 1, 0)
+                spread_table(tab_k, tabx_k, tt + 1, 1)

@@ -78,11 +78,11 @@ def tile_selfattn_pa_kernel(tc, x, wq_words, wq_scales, wk_words, wk_scales, wv_
 
         def load_table(tab, cos, sin, tt):
             nc.sync.dma_start(out=tab[tt][:, 0, 0, :], in_=cos[tt * P:(tt + 1) * P, :])
-            nc.sync.dma_start(out=tab[tt][:, 1, 0, :], in_=sin[tt * P:(tt + 1) * P, :])
+            nc.sync.dma_start(out=tab[tt][:, 1, 1, :], in_=sin[tt * P:(tt + 1) * P, :])
 
         def prep_table(tab, tt):
-            nc.scalar.copy(out=tab[tt][:, 1, 1, :], in_=tab[tt][:, 0, 0, :])
-            nc.scalar.mul(out=tab[tt][:, 0, 1, :], in_=tab[tt][:, 1, 0, :], mul=-1.0)
+            nc.scalar.copy(out=tab[tt][:, 0, 1, :], in_=tab[tt][:, 0, 0, :])
+            nc.scalar.mul(out=tab[tt][:, 1, 0, :], in_=tab[tt][:, 1, 1, :], mul=-1.0)
 
         load_x(0)
         load_x(1)
@@ -147,7 +147,7 @@ def tile_selfattn_pa_kernel(tc, x, wq_words, wq_scales, wk_words, wk_scales, wv_
                 factors = tabx[:, :, 512 * j:512 * (j + 1)].rearrange("p w (i e) -> p w i e", e=2)
             nc.vector.tensor_tensor(
                 out=at[:, :, off:off + 512].rearrange("p w (i e) -> p w i e", e=2),
-                in0=acc[:].rearrange("p (i w) -> p w i", w=2).unsqueeze(3).to_broadcast([P, 2, 256, 2]),
+                in0=acc[:].rearrange("p (i e) -> p i e", e=2).unsqueeze(1).to_broadcast([P, 2, 256, 2]),
                 in1=factors,
                 op=MULT)
 
@@ -181,13 +181,17 @@ def tile_selfattn_pa_kernel(tc, x, wq_words, wq_scales, wk_words, wk_scales, wv_
 
             res = work.tile([P, NR], F32, name="res", tag="res")
             if not last:
-                nc.gpsimd.tensor_tensor(out=res[:], in0=at[:, 0, :], in1=at[:, 1, :], op=ADD)
+                nc.gpsimd.tensor_tensor(out=res[:].rearrange("p (i e) -> p i e", e=2),
+                                        in0=at[:, 0, :].rearrange("p (i e) -> p i e", e=2),
+                                        in1=at[:, 1, :].rearrange("p (i e) -> p i e", e=2)[:, :, ::-1], op=ADD)
                 nc.sync.dma_start(out=out_q[b, rows, :], in_=res[:, 0:NQ])
                 nc.sync.dma_start(out=out_k[b, rows, :], in_=res[:, NQ:NR])
             else:
                 for j in range(3):
                     cols = slice(512 * j, 512 * (j + 1))
-                    nc.vector.tensor_tensor(out=res[:, cols], in0=at[:, 0, cols], in1=at[:, 1, cols], op=ADD)
+                    nc.vector.tensor_tensor(out=res[:, cols].rearrange("p (i e) -> p i e", e=2),
+                                            in0=at[:, 0, cols].rearrange("p (i e) -> p i e", e=2),
+                                            in1=at[:, 1, cols].rearrange("p (i e) -> p i e", e=2)[:, :, ::-1], op=ADD)
                     if j < 2:
                         nc.sync.dma_start(out=out_q[b, rows, cols], in_=res[:, cols])
                     else:

@@ -173,6 +173,9 @@ def tile_selfattn_pa_kernel(tc, x, wq_words, wq_scales, wk_words, wk_scales, wv_
                 quantize(2)
             acc = project(t, "k", 0)
             products(acc, at, NQ, tab_k[tt], tabx_k[tt], 0)
+            if t == 1:
+                turn(4)
+                turn(5)
 
             acc = project(t, "v", 0)
             res_v = work.tile([P, NK], F32, name="res_v", tag="res_v")
@@ -180,24 +183,28 @@ def tile_selfattn_pa_kernel(tc, x, wq_words, wq_scales, wk_words, wk_scales, wv_
             nc.scalar.dma_start(out=out_v[b, rows, :], in_=res_v[:])
 
             res = work.tile([P, NR], F32, name="res", tag="res")
-            if not last:
+            if t < NTILES - 2:
                 nc.gpsimd.tensor_tensor(out=res[:].rearrange("p (i e) -> p i e", e=2),
                                         in0=at[:, 0, :].rearrange("p (i e) -> p i e", e=2),
                                         in1=at[:, 1, :].rearrange("p (i e) -> p i e", e=2)[:, :, ::-1], op=ADD)
                 nc.sync.dma_start(out=out_q[b, rows, :], in_=res[:, 0:NQ])
                 nc.sync.dma_start(out=out_k[b, rows, :], in_=res[:, NQ:NR])
             else:
-                for j in range(3):
+                todo = [(nc.gpsimd, at, res, b, rows, j) for j in range(2)]
+                if last:
+                    todo = [held] + [(nc.vector, at, res, b, rows, j) for j in range(3)]
+                held = (nc.vector, at, res, b, rows, 2)
+                for adder, at_a, res_a, b_a, rows_a, j in todo:
                     cols = slice(512 * j, 512 * (j + 1))
-                    nc.vector.tensor_tensor(out=res[:, cols].rearrange("p (i e) -> p i e", e=2),
-                                            in0=at[:, 0, cols].rearrange("p (i e) -> p i e", e=2),
-                                            in1=at[:, 1, cols].rearrange("p (i e) -> p i e", e=2)[:, :, ::-1], op=ADD)
+                    adder.tensor_tensor(out=res_a[:, cols].rearrange("p (i e) -> p i e", e=2),
+                                        in0=at_a[:, 0, cols].rearrange("p (i e) -> p i e", e=2),
+                                        in1=at_a[:, 1, cols].rearrange("p (i e) -> p i e", e=2)[:, :, ::-1], op=ADD)
                     if j < 2:
-                        nc.sync.dma_start(out=out_q[b, rows, cols], in_=res[:, cols])
+                        nc.sync.dma_start(out=out_q[b_a, rows_a, cols], in_=res_a[:, cols])
                     else:
-                        nc.sync.dma_start(out=out_k[b, rows, :], in_=res[:, cols])
+                        nc.sync.dma_start(out=out_k[b_a, rows_a, :], in_=res_a[:, cols])
 
-            if b in (0, 1) and tt + 1 < TT:
+            if b in (0, 1) and tt + 1 < TT and t > 0:
                 turn(4 * tt + 4 + 2 * b)
                 turn(4 * tt + 5 + 2 * b)
             if b == 2 and tt + 1 < TT:

@@ -151,6 +151,58 @@ def tile_selfattn_pa_kernel(tc, x, wq_words, wq_scales, wk_words, wk_scales, wv_
                 in1=factors,
                 op=MULT)
 
+        def new_at():
+            return work.tile([P, 2, NR], F32, name="at", tag="at", bufs=5)
+
+        def q_bank(t, at, j):
+            acc = project(t, "q", j)
+            products(acc, at, 512 * j, tab_q[t // B], tabx_q[t // B], j)
+
+        def k_bank(t, at):
+            acc = project(t, "k", 0)
+            products(acc, at, NQ, tab_k[t // B], tabx_k[t // B], 0)
+
+        def v_bank(t):
+            tt, b = divmod(t, B)
+            acc = project(t, "v", 0)
+            res_v = work.tile([P, NK], F32, name="res_v", tag="res_v")
+            nc.scalar.copy(out=res_v[:], in_=acc[:])
+            nc.scalar.dma_start(out=out_v[b, tt * P:(tt + 1) * P, :], in_=res_v[:])
+
+        def add_piece(adder, t, at, res, j):
+            tt, b = divmod(t, B)
+            rows = slice(tt * P, (tt + 1) * P)
+            cols = slice(512 * j, 512 * (j + 1))
+            adder.tensor_tensor(out=res[:, cols].rearrange("p (i e) -> p i e", e=2),
+                                in0=at[:, 0, cols].rearrange("p (i e) -> p i e", e=2),
+                                in1=at[:, 1, cols].rearrange("p (i e) -> p i e", e=2)[:, :, ::-1], op=ADD)
+            if j < 2:
+                nc.sync.dma_start(out=out_q[b, rows, cols], in_=res[:, cols])
+            else:
+                nc.sync.dma_start(out=out_k[b, rows, :], in_=res[:, cols])
+
+        held = []
+
+        def finish(t, at):
+            tt, b = divmod(t, B)
+            rows = slice(tt * P, (tt + 1) * P)
+            res = work.tile([P, NR], F32, name="res", tag="res", bufs=4)
+            if t < NTILES - 2:
+                nc.gpsimd.tensor_tensor(out=res[:].rearrange("p (i e) -> p i e", e=2),
+                                        in0=at[:, 0, :].rearrange("p (i e) -> p i e", e=2),
+                                        in1=at[:, 1, :].rearrange("p (i e) -> p i e", e=2)[:, :, ::-1], op=ADD)
+                nc.sync.dma_start(out=out_q[b, rows, :], in_=res[:, 0:NQ])
+                nc.sync.dma_start(out=out_k[b, rows, :], in_=res[:, NQ:NR])
+            elif t == NTILES - 2:
+                add_piece(nc.gpsimd, t, at, res, 0)
+                add_piece(nc.gpsimd, t, at, res, 1)
+                held.append((t, at, res))
+            else:
+                t_h, at_h, res_h = held[0]
+                add_piece(nc.vector, t_h, at_h, res_h, 2)
+                for j in range(3):
+                    add_piece(nc.vector, t, at, res, j)
+
         turn(0)
         quantize(0)
         turn(1)
@@ -160,60 +212,30 @@ def tile_selfattn_pa_kernel(tc, x, wq_words, wq_scales, wk_words, wk_scales, wv_
 
         for t in range(NTILES):
             tt, b = divmod(t, B)
-            rows = slice(tt * P, (tt + 1) * P)
-            last = t == NTILES - 1
-
-            at = work.tile([P, 2, NR], F32, name="at", tag="at")
-            for j in range(2):
-                acc = project(t, "q", j)
-                products(acc, at, 512 * j, tab_q[tt], tabx_q[tt], j)
+            at = new_at()
+            q_bank(t, at, 0)
+            q_bank(t, at, 1)
             if t == 0:
                 turn(2)
                 turn(3)
                 quantize(2)
-            acc = project(t, "k", 0)
-            products(acc, at, NQ, tab_k[tt], tabx_k[tt], 0)
+            k_bank(t, at)
             if t == 1:
                 turn(4)
                 turn(5)
-
-            acc = project(t, "v", 0)
-            res_v = work.tile([P, NK], F32, name="res_v", tag="res_v")
-            nc.scalar.copy(out=res_v[:], in_=acc[:])
-            nc.scalar.dma_start(out=out_v[b, rows, :], in_=res_v[:])
-
-            res = work.tile([P, NR], F32, name="res", tag="res")
-            if t < NTILES - 2:
-                nc.gpsimd.tensor_tensor(out=res[:].rearrange("p (i e) -> p i e", e=2),
-                                        in0=at[:, 0, :].rearrange("p (i e) -> p i e", e=2),
-                                        in1=at[:, 1, :].rearrange("p (i e) -> p i e", e=2)[:, :, ::-1], op=ADD)
-                nc.sync.dma_start(out=out_q[b, rows, :], in_=res[:, 0:NQ])
-                nc.sync.dma_start(out=out_k[b, rows, :], in_=res[:, NQ:NR])
-            else:
-                todo = [(nc.gpsimd, at, res, b, rows, j) for j in range(2)]
-                if last:
-                    todo = [held] + [(nc.vector, at, res, b, rows, j) for j in range(3)]
-                held = (nc.vector, at, res, b, rows, 2)
-                for adder, at_a, res_a, b_a, rows_a, j in todo:
-                    cols = slice(512 * j, 512 * (j + 1))
-                    adder.tensor_tensor(out=res_a[:, cols].rearrange("p (i e) -> p i e", e=2),
-                                        in0=at_a[:, 0, cols].rearrange("p (i e) -> p i e", e=2),
-                                        in1=at_a[:, 1, cols].rearrange("p (i e) -> p i e", e=2)[:, :, ::-1], op=ADD)
-                    if j < 2:
-                        nc.sync.dma_start(out=out_q[b_a, rows_a, cols], in_=res_a[:, cols])
-                    else:
-                        nc.sync.dma_start(out=out_k[b_a, rows_a, :], in_=res_a[:, cols])
-
-            if b in (0, 1) and tt + 1 < TT and t > 0:
+            v_bank(t)
+            finish(t, at)
+            more = tt + 1 < TT
+            if more and b in (0, 1) and t > 0:
                 turn(4 * tt + 4 + 2 * b)
                 turn(4 * tt + 5 + 2 * b)
-            if b == 2 and tt + 1 < TT:
+            if more and b == 2:
                 quantize(tt + 3)
-            if b == 1 and tt + 1 < TT:
+            if more and b == 1:
                 prep_table(tab_q, tt + 1)
                 prep_table(tab_k, tt + 1)
                 spread_table(tab_q, tabx_q, tt + 1, 0)
-            if b == 2 and tt + 1 < TT:
+            if more and b == 2:
                 spread_table(tab_q, tabx_q, tt + 1, 1)
                 spread_table(tab_k, tabx_k, tt + 1, 0)
                 spread_table(tab_k, tabx_k, tt + 1, 1)

@@ -220,13 +220,13 @@ def tile_selfattn_pa_kernel(tc, x, wq_words, wq_scales, wk_words, wk_scales, wv_
                 turn(3)
                 quantize(2)
             k_bank(t, at)
-            if t == 1:
-                turn(4)
-                turn(5)
+            if t in (1, 2):
+                turn(2 * t + 2)
+                turn(2 * t + 3)
             v_bank(t)
             finish(t, at)
             more = tt + 1 < TT
-            if more and b in (0, 1) and t > 0:
+            if more and b in (0, 1) and t > 1:
                 turn(4 * tt + 4 + 2 * b)
                 turn(4 * tt + 5 + 2 * b)
             if more and b == 2:

@@ -182,6 +182,11 @@ def tile_selfattn_pa_kernel(tc, x, wq_words, wq_scales, wk_words, wk_scales, wv_
                 nc.sync.dma_start(out=out_k[b, rows, :], in_=res[:, cols])
 
         held = []
+        order = keep.tile([P, 1], U32, name="order")
+
+        def hold_gpsimd(qi):
+            nc.gpsimd.tensor_copy(out=order[:], in_=codes_of[qi][0][:, 0:1])
+
 
         def finish(t, at):
             tt, b = divmod(t, B)
@@ -212,6 +217,7 @@ def tile_selfattn_pa_kernel(tc, x, wq_words, wq_scales, wk_words, wk_scales, wv_
 
         for t in range(NTILES):
             tt, b = divmod(t, B)
+            more = tt + 1 < TT
             at = new_at()
             q_bank(t, at, 0)
             q_bank(t, at, 1)
@@ -219,23 +225,36 @@ def tile_selfattn_pa_kernel(tc, x, wq_words, wq_scales, wk_words, wk_scales, wv_
                 turn(2)
                 turn(3)
                 quantize(2)
+            if t == 2:
+                turn(6)
+                turn(7)
             k_bank(t, at)
-            if t in (1, 2):
-                turn(2 * t + 2)
-                turn(2 * t + 3)
+            if t == 1:
+                turn(4)
+                turn(5)
+            if t == 2:
+                quantize(3)
+                hold_gpsimd(3)
             v_bank(t)
             finish(t, at)
-            more = tt + 1 < TT
-            if more and b in (0, 1) and t > 1:
+            if t == 2:
+                prep_table(tab_q, 1)
+                spread_table(tab_q, tabx_q, 1, 0)
+                spread_table(tab_q, tabx_q, 1, 1)
+                prep_table(tab_k, 1)
+                spread_table(tab_k, tabx_k, 1, 0)
+                spread_table(tab_k, tabx_k, 1, 1)
+            inner = more and tt > 0
+            if inner and b in (0, 1):
                 turn(4 * tt + 4 + 2 * b)
                 turn(4 * tt + 5 + 2 * b)
-            if more and b == 2:
+            if inner and b == 2:
                 quantize(tt + 3)
-            if more and b == 1:
+            if inner and b == 1:
                 prep_table(tab_q, tt + 1)
                 prep_table(tab_k, tt + 1)
                 spread_table(tab_q, tabx_q, tt + 1, 0)
-            if more and b == 2:
+            if inner and b == 2:
                 spread_table(tab_q, tabx_q, tt + 1, 1)
                 spread_table(tab_k, tabx_k, tt + 1, 0)
                 spread_table(tab_k, tabx_k, tt + 1, 1)

@@ -225,13 +225,10 @@ def tile_selfattn_pa_kernel(tc, x, wq_words, wq_scales, wk_words, wk_scales, wv_
                 turn(2)
                 turn(3)
                 quantize(2)
-            if t == 2:
-                turn(6)
-                turn(7)
             k_bank(t, at)
-            if t == 1:
-                turn(4)
-                turn(5)
+            if t in (1, 2):
+                turn(2 * t + 2)
+                turn(2 * t + 3)
             if t == 2:
                 quantize(3)
                 hold_gpsimd(3)

@@ -24,6 +24,9 @@ FLOPS = 2 * B * T * D * (NQ + 2 * NK)
 XLOADS = [[0], [1]] + [[n, n + 1] for n in range(2, NTILES, 2)]
 QGROUPS = [[0], [1], [2, 3], [4, 5, 6, 7], [8, 9, 10, 11], [12, 13, 14, 15]]
 NR = NQ + NK
+HOLDS = {2: 3, 6: 4, 10: 5}
+HELD_BY = {3: 2, 4: 6, 5: 10}
+SLOT = 4096 * 2
 
 
 def tile_selfattn_pa_kernel(tc, x, wq_words, wq_scales, wk_words, wk_scales, wv_words, wv_scales,
@@ -32,6 +35,7 @@ def tile_selfattn_pa_kernel(tc, x, wq_words, wq_scales, wk_words, wk_scales, wv_
     with ExitStack() as ctx:
         keep = ctx.enter_context(tc.tile_pool(name="keep", bufs=1))
         work = ctx.enter_context(tc.tile_pool(name="work", bufs=3))
+        share = ctx.enter_context(tc.tile_pool(name="share", bufs=1))
         psum = ctx.enter_context(tc.psum_pool(name="psum", bufs=2))
         ctx.enter_context(tc.manual_schedule())
 
@@ -78,11 +82,11 @@ def tile_selfattn_pa_kernel(tc, x, wq_words, wq_scales, wk_words, wk_scales, wv_
 
         def load_table(tab, cos, sin, tt):
             nc.sync.dma_start(out=tab[tt][:, 0, 0, :], in_=cos[tt * P:(tt + 1) * P, :])
-            nc.sync.dma_start(out=tab[tt][:, 1, 1, :], in_=sin[tt * P:(tt + 1) * P, :])
+            nc.sync.dma_start(out=tab[tt][:, 1, 0, :], in_=sin[tt * P:(tt + 1) * P, :])
 
         def prep_table(tab, tt):
-            nc.scalar.copy(out=tab[tt][:, 0, 1, :], in_=tab[tt][:, 0, 0, :])
-            nc.scalar.mul(out=tab[tt][:, 1, 0, :], in_=tab[tt][:, 1, 1, :], mul=-1.0)
+            nc.scalar.copy(out=tab[tt][:, 1, 1, :], in_=tab[tt][:, 0, 0, :])
+            nc.scalar.mul(out=tab[tt][:, 0, 1, :], in_=tab[tt][:, 1, 0, :], mul=-1.0)
 
         load_x(0)
         load_x(1)
@@ -107,7 +111,10 @@ def tile_selfattn_pa_kernel(tc, x, wq_words, wq_scales, wk_words, wk_scales, wv_
 
         def turn(t):
             qi, a = group_of[t]
-            if a == 0:
+            if a == 0 and qi in HELD_BY:
+                grouped_of[qi] = share.tile([P, 4096], BF16, name="wide%d" % (qi % 2), offset=(qi % 2) * SLOT,
+                                            align_bytes=64)
+            elif a == 0:
                 grouped_of[qi] = work.tile([P, len(QGROUPS[qi]) * 1024], BF16, name="grouped", tag="grouped",
                                            bufs=2, align_bytes=64)
             li, xa = x_of[t]
@@ -140,27 +147,27 @@ def tile_selfattn_pa_kernel(tc, x, wq_words, wq_scales, wk_words, wk_scales, wv_
                                     start=(g == 0), stop=(g == G - 1))
             return acc
 
-        def products(acc, at, off, tab, tabx, j):
+        def products(acc, at, bank, tab, tabx, j):
             if tabx is None:
                 factors = tab[:, :, :, 256 * j:256 * (j + 1)].rearrange("p w e i -> p w i e")
             else:
                 factors = tabx[:, :, 512 * j:512 * (j + 1)].rearrange("p w (i e) -> p w i e", e=2)
             nc.vector.tensor_tensor(
-                out=at[:, :, off:off + 512].rearrange("p w (i e) -> p w i e", e=2),
-                in0=acc[:].rearrange("p (i e) -> p i e", e=2).unsqueeze(1).to_broadcast([P, 2, 256, 2]),
+                out=at[:, bank, :, :].rearrange("p w (i e) -> p w i e", e=2),
+                in0=acc[:].rearrange("p (i w) -> p w i", w=2).unsqueeze(3).to_broadcast([P, 2, 256, 2]),
                 in1=factors,
                 op=MULT)
 
         def new_at():
-            return work.tile([P, 2, NR], F32, name="at", tag="at", bufs=5)
+            return work.tile([P, 3, 2, 512], F32, name="at", tag="at", bufs=5)
 
         def q_bank(t, at, j):
             acc = project(t, "q", j)
-            products(acc, at, 512 * j, tab_q[t // B], tabx_q[t // B], j)
+            products(acc, at, j, tab_q[t // B], tabx_q[t // B], j)
 
         def k_bank(t, at):
             acc = project(t, "k", 0)
-            products(acc, at, NQ, tab_k[t // B], tabx_k[t // B], 0)
+            products(acc, at, 2, tab_k[t // B], tabx_k[t // B], 0)
 
         def v_bank(t):
             tt, b = divmod(t, B)
@@ -173,29 +180,25 @@ def tile_selfattn_pa_kernel(tc, x, wq_words, wq_scales, wk_words, wk_scales, wv_
             tt, b = divmod(t, B)
             rows = slice(tt * P, (tt + 1) * P)
             cols = slice(512 * j, 512 * (j + 1))
-            adder.tensor_tensor(out=res[:, cols].rearrange("p (i e) -> p i e", e=2),
-                                in0=at[:, 0, cols].rearrange("p (i e) -> p i e", e=2),
-                                in1=at[:, 1, cols].rearrange("p (i e) -> p i e", e=2)[:, :, ::-1], op=ADD)
+            adder.tensor_tensor(out=res[:, cols], in0=at[:, j, 0, :], in1=at[:, j, 1, :], op=ADD)
             if j < 2:
                 nc.sync.dma_start(out=out_q[b, rows, cols], in_=res[:, cols])
             else:
                 nc.sync.dma_start(out=out_k[b, rows, :], in_=res[:, cols])
 
         held = []
-        order = keep.tile([P, 1], U32, name="order")
-
-        def hold_gpsimd(qi):
-            nc.gpsimd.tensor_copy(out=order[:], in_=codes_of[qi][0][:, 0:1])
-
 
         def finish(t, at):
             tt, b = divmod(t, B)
             rows = slice(tt * P, (tt + 1) * P)
-            res = work.tile([P, NR], F32, name="res", tag="res", bufs=4)
+            if t in HOLDS:
+                res = share.tile([P, NR], F32, name="held%d" % (HOLDS[t] % 2), offset=(HOLDS[t] % 2) * SLOT,
+                                 align_bytes=64)
+            else:
+                res = work.tile([P, NR], F32, name="res", tag="res", bufs=4)
             if t < NTILES - 2:
-                nc.gpsimd.tensor_tensor(out=res[:].rearrange("p (i e) -> p i e", e=2),
-                                        in0=at[:, 0, :].rearrange("p (i e) -> p i e", e=2),
-                                        in1=at[:, 1, :].rearrange("p (i e) -> p i e", e=2)[:, :, ::-1], op=ADD)
+                nc.gpsimd.tensor_tensor(out=res[:].rearrange("p (j c) -> p j c", j=3),
+                                        in0=at[:, :, 0, :], in1=at[:, :, 1, :], op=ADD)
                 nc.sync.dma_start(out=out_q[b, rows, :], in_=res[:, 0:NQ])
                 nc.sync.dma_start(out=out_k[b, rows, :], in_=res[:, NQ:NR])
             elif t == NTILES - 2:
@@ -229,9 +232,8 @@ def tile_selfattn_pa_kernel(tc, x, wq_words, wq_scales, wk_words, wk_scales, wv_
             if t in (1, 2):
                 turn(2 * t + 2)
                 turn(2 * t + 3)
-            if t == 2:
-                quantize(3)
-                hold_gpsimd(3)
+            if t in HOLDS:
+                quantize(HOLDS[t])
             v_bank(t)
             finish(t, at)
             if t == 2:
@@ -245,8 +247,6 @@ def tile_selfattn_pa_kernel(tc, x, wq_words, wq_scales, wk_words, wk_scales, wv_
             if inner and b in (0, 1):
                 turn(4 * tt + 4 + 2 * b)
                 turn(4 * tt + 5 + 2 * b)
-            if inner and b == 2:
-                quantize(tt + 3)
             if inner and b == 1:
                 prep_table(tab_q, tt + 1)
                 prep_table(tab_k, tt + 1)

@@ -26,6 +26,7 @@ QGROUPS = [[0], [1], [2, 3], [4, 5, 6, 7], [8, 9, 10, 11], [12, 13, 14, 15]]
 NR = NQ + NK
 HOLDS = {2: 3, 6: 4, 10: 5}
 HELD_BY = {3: 2, 4: 6, 5: 10}
+TENSOR_ADDS = (5, 9, 13)
 SLOT = 4096 * 2
 
 
@@ -187,6 +188,17 @@ def tile_selfattn_pa_kernel(tc, x, wq_words, wq_scales, wk_words, wk_scales, wv_
                 nc.sync.dma_start(out=out_k[b, rows, :], in_=res[:, cols])
 
         held = []
+        waiting = {}
+
+        def tensor_add(t):
+            tt, b = divmod(t, B)
+            at = waiting[t]
+            total = psum.tile([P, 512], F32, name="acc", tag="acc", bufs=6)
+            nc.tensor.matmul(out=total[:], lhsT=ident[:], rhs=at[:, 2, 0, :], start=True, stop=False)
+            nc.tensor.matmul(out=total[:], lhsT=ident[:], rhs=at[:, 2, 1, :], start=False, stop=True)
+            res_k = work.tile([P, NK], F32, name="res_k", tag="res_k", bufs=2)
+            nc.scalar.copy(out=res_k[:], in_=total[:])
+            nc.sync.dma_start(out=out_k[b, tt * P:(tt + 1) * P, :], in_=res_k[:])
 
         def finish(t, at):
             tt, b = divmod(t, B)
@@ -196,7 +208,12 @@ def tile_selfattn_pa_kernel(tc, x, wq_words, wq_scales, wk_words, wk_scales, wv_
                                  align_bytes=64)
             else:
                 res = work.tile([P, NR], F32, name="res", tag="res", bufs=4)
-            if t < NTILES - 2:
+            if t in TENSOR_ADDS:
+                nc.gpsimd.tensor_tensor(out=res[:, 0:NQ].rearrange("p (j c) -> p j c", j=2),
+                                        in0=at[:, 0:2, 0, :], in1=at[:, 0:2, 1, :], op=ADD)
+                nc.sync.dma_start(out=out_q[b, rows, :], in_=res[:, 0:NQ])
+                waiting[t] = at
+            elif t < NTILES - 2:
                 nc.gpsimd.tensor_tensor(out=res[:].rearrange("p (j c) -> p j c", j=3),
                                         in0=at[:, :, 0, :], in1=at[:, :, 1, :], op=ADD)
                 nc.sync.dma_start(out=out_q[b, rows, :], in_=res[:, 0:NQ])
@@ -236,6 +253,8 @@ def tile_selfattn_pa_kernel(tc, x, wq_words, wq_scales, wk_words, wk_scales, wv_
                 quantize(HOLDS[t])
             v_bank(t)
             finish(t, at)
+            if t - 1 in TENSOR_ADDS:
+                tensor_add(t - 1)
             if t == 2:
                 prep_table(tab_q, 1)
                 spread_table(tab_q, tabx_q, 1, 0)

@@ -26,7 +26,7 @@ QGROUPS = [[0], [1], [2, 3], [4, 5, 6, 7], [8, 9, 10, 11], [12, 13, 14, 15]]
 NR = NQ + NK
 HOLDS = {2: 3, 6: 4, 10: 5}
 HELD_BY = {3: 2, 4: 6, 5: 10}
-TENSOR_ADDS = (5, 9, 13)
+TENSOR_ADDS = (5, 9, 13, 14)
 SLOT = 4096 * 2
 
 
@@ -187,7 +187,6 @@ def tile_selfattn_pa_kernel(tc, x, wq_words, wq_scales, wk_words, wk_scales, wv_
             else:
                 nc.sync.dma_start(out=out_k[b, rows, :], in_=res[:, cols])
 
-        held = []
         waiting = {}
 
         def tensor_add(t):
@@ -198,7 +197,7 @@ def tile_selfattn_pa_kernel(tc, x, wq_words, wq_scales, wk_words, wk_scales, wv_
             nc.tensor.matmul(out=total[:], lhsT=ident[:], rhs=at[:, 2, 1, :], start=False, stop=True)
             res_k = work.tile([P, NK], F32, name="res_k", tag="res_k", bufs=2)
             nc.scalar.copy(out=res_k[:], in_=total[:])
-            nc.sync.dma_start(out=out_k[b, tt * P:(tt + 1) * P, :], in_=res_k[:])
+            nc.scalar.dma_start(out=out_k[b, tt * P:(tt + 1) * P, :], in_=res_k[:])
 
         def finish(t, at):
             tt, b = divmod(t, B)
@@ -208,7 +207,7 @@ def tile_selfattn_pa_kernel(tc, x, wq_words, wq_scales, wk_words, wk_scales, wv_
                                  align_bytes=64)
             else:
                 res = work.tile([P, NR], F32, name="res", tag="res", bufs=4)
-            if t in TENSOR_ADDS:
+            if t in TENSOR_ADDS and t < NTILES - 2:
                 nc.gpsimd.tensor_tensor(out=res[:, 0:NQ].rearrange("p (j c) -> p j c", j=2),
                                         in0=at[:, 0:2, 0, :], in1=at[:, 0:2, 1, :], op=ADD)
                 nc.sync.dma_start(out=out_q[b, rows, :], in_=res[:, 0:NQ])
@@ -221,12 +220,11 @@ def tile_selfattn_pa_kernel(tc, x, wq_words, wq_scales, wk_words, wk_scales, wv_
             elif t == NTILES - 2:
                 add_piece(nc.gpsimd, t, at, res, 0)
                 add_piece(nc.gpsimd, t, at, res, 1)
-                held.append((t, at, res))
+                waiting[t] = at
             else:
-                t_h, at_h, res_h = held[0]
-                add_piece(nc.vector, t_h, at_h, res_h, 2)
-                for j in range(3):
-                    add_piece(nc.vector, t, at, res, j)
+                add_piece(nc.gpsimd, t, at, res, 0)
+                add_piece(nc.vector, t, at, res, 1)
+                add_piece(nc.vector, t, at, res, 2)
 
         turn(0)
         quantize(0)
@@ -251,7 +249,10 @@ def tile_selfattn_pa_kernel(tc, x, wq_words, wq_scales, wk_words, wk_scales, wv_
                 turn(2 * t + 3)
             if t in HOLDS:
                 quantize(HOLDS[t])
-            v_bank(t)
+            if t < NTILES - 2:
+                v_bank(t)
+            if t in (NTILES - 4, NTILES - 3):
+                v_bank(t + 2)
             finish(t, at)
             if t - 1 in TENSOR_ADDS:
                 tensor_add(t - 1)

@@ -112,7 +112,9 @@ def tile_selfattn_pa_kernel(tc, x, wq_words, wq_scales, wk_words, wk_scales, wv_
 
         def turn(t):
             qi, a = group_of[t]
-            if a == 0 and qi in HELD_BY:
+            if a == 0 and qi == 2:
+                grouped_of[qi] = share.tile([P, 2048], BF16, name="pair", offset=0, align_bytes=64)
+            elif a == 0 and qi in HELD_BY:
                 grouped_of[qi] = share.tile([P, 4096], BF16, name="wide%d" % (qi % 2), offset=(qi % 2) * SLOT,
                                             align_bytes=64)
             elif a == 0:
@@ -233,18 +235,38 @@ def tile_selfattn_pa_kernel(tc, x, wq_words, wq_scales, wk_words, wk_scales, wv_
         prep_table(tab_q, 0)
         prep_table(tab_k, 0)
 
-        for t in range(NTILES):
+        at_0 = new_at()
+        at_1 = new_at()
+        q_bank(0, at_0, 0)
+        q_bank(0, at_0, 1)
+        k_bank(0, at_0)
+        res_0 = work.tile([P, NR], F32, name="res", tag="res", bufs=4)
+        nc.gpsimd.tensor_tensor(out=res_0[:, 0:NQ].rearrange("p (j c) -> p j c", j=2),
+                                in0=at_0[:, 0:2, 0, :], in1=at_0[:, 0:2, 1, :], op=ADD)
+        nc.sync.dma_start(out=out_q[0, 0:P, :], in_=res_0[:, 0:NQ])
+        q_bank(1, at_1, 0)
+        q_bank(1, at_1, 1)
+        turn(2)
+        turn(3)
+        quantize(2)
+        held_k = share.tile([P, NK], F32, name="held_k", offset=0, align_bytes=64)
+        nc.gpsimd.tensor_tensor(out=held_k[:], in0=at_0[:, 2, 0, :], in1=at_0[:, 2, 1, :], op=ADD)
+        nc.sync.dma_start(out=out_k[0, 0:P, :], in_=held_k[:])
+        v_bank(0)
+        k_bank(1, at_1)
+        turn(4)
+        turn(5)
+        v_bank(1)
+        finish(1, at_1)
+
+        for t in range(2, NTILES):
             tt, b = divmod(t, B)
             more = tt + 1 < TT
             at = new_at()
             q_bank(t, at, 0)
             q_bank(t, at, 1)
-            if t == 0:
-                turn(2)
-                turn(3)
-                quantize(2)
             k_bank(t, at)
-            if t in (1, 2):
+            if t == 2:
                 turn(2 * t + 2)
                 turn(2 * t + 3)
             if t in HOLDS:

@@ -93,9 +93,9 @@ def tile_selfattn_pa_kernel(tc, x, wq_words, wq_scales, wk_words, wk_scales, wv_
         load_x(1)
         load_weight("q", wq_words, wq_scales)
         load_table(tab_q, cos_q, sin_q, 0)
-        load_x(2)
         load_weight("k", wk_words, wk_scales)
         load_table(tab_k, cos_k, sin_k, 0)
+        load_x(2)
         load_weight("v", wv_words, wv_scales)
         for tt in range(1, TT):
             load_x(2 * tt + 1)
@@ -252,8 +252,8 @@ def tile_selfattn_pa_kernel(tc, x, wq_words, wq_scales, wk_words, wk_scales, wv_
         held_k = share.tile([P, NK], F32, name="held_k", offset=0, align_bytes=64)
         nc.gpsimd.tensor_tensor(out=held_k[:], in0=at_0[:, 2, 0, :], in1=at_0[:, 2, 1, :], op=ADD)
         nc.sync.dma_start(out=out_k[0, 0:P, :], in_=held_k[:])
-        v_bank(0)
         k_bank(1, at_1)
+        v_bank(0)
         turn(4)
         turn(5)
         v_bank(1)

@@ -27,6 +27,7 @@ NR = NQ + NK
 HOLDS = {2: 3, 6: 4, 10: 5}
 HELD_BY = {3: 2, 4: 6, 5: 10}
 TENSOR_ADDS = (5, 9, 13, 14)
+WARM_FIRST, WARM_SECOND = 4, 2
 SLOT = 4096 * 2
 
 
@@ -49,8 +50,15 @@ def tile_selfattn_pa_kernel(tc, x, wq_words, wq_scales, wk_words, wk_scales, wv_
         warm = keep.tile([P, 2], F32, name="warm")
         nc.vector.memset(warm[:, 0:1], 0.0)
         nc.scalar.copy(out=warm[:, 1:2], in_=warm[:, 0:1])
+        zeros = keep.tile([P, 512], BF16, name="zeros")
+        nc.gpsimd.memset(zeros[:], 0.0)
         ident = keep.tile([P, P], F32, name="ident")
         make_identity(nc, ident[:])
+
+        def idle_matmuls(n):
+            for i in range(n):
+                waste = psum.tile([P, 512], F32, name="acc", tag="acc", bufs=6)
+                nc.tensor.matmul(out=waste[:], lhsT=zeros[:, 0:P], rhs=zeros[:], start=True, stop=True)
 
         x_of = {}
         x_sb = []
@@ -228,11 +236,14 @@ def tile_selfattn_pa_kernel(tc, x, wq_words, wq_scales, wk_words, wk_scales, wv_
                 add_piece(nc.vector, t, at, res, 1)
                 add_piece(nc.vector, t, at, res, 2)
 
+        idle_matmuls(WARM_FIRST)
         turn(0)
         quantize(0)
         turn(1)
         quantize(1)
-        prep_table(tab_q, 0)
+        idle_matmuls(WARM_SECOND)
+        nc.vector.tensor_copy(out=tab_q[0][:, 1, 1, :], in_=tab_q[0][:, 0, 0, :])
+        nc.vector.tensor_scalar_mul(out=tab_q[0][:, 0, 1, :], in0=tab_q[0][:, 1, 0, :], scalar1=-1.0)
         prep_table(tab_k, 0)
 
         at_0 = new_at()

@@ -199,14 +199,27 @@ def tile_selfattn_pa_kernel(tc, x, wq_words, wq_scales, wk_words, wk_scales, wv_
 
         waiting = {}
 
-        def tensor_add(t):
-            tt, b = divmod(t, B)
+        turned_of = {}
+
+        def tensor_add_first(t):
             at = waiting[t]
-            total = psum.tile([P, 512], F32, name="acc", tag="acc", bufs=6)
-            nc.tensor.matmul(out=total[:], lhsT=ident[:], rhs=at[:, 2, 0, :], start=True, stop=False)
-            nc.tensor.matmul(out=total[:], lhsT=ident[:], rhs=at[:, 2, 1, :], start=False, stop=True)
+            turned = psum.tile([P, 512], F32, name="acc", tag="acc", bufs=6)
+            for c in range(4):
+                cols = slice(c * P, (c + 1) * P)
+                for w in range(2):
+                    nc.tensor.matmul(out=turned[:, cols], lhsT=at[:, 2, w, cols], rhs=ident[:], is_transpose=True,
+                                     start=(w == 0), stop=(w == 1))
+            turned_of[t] = work.tile([P, NK], F32, name="turned", tag="turned", bufs=2)
+            nc.scalar.copy(out=turned_of[t][:], in_=turned[:])
+
+        def tensor_add_second(t):
+            tt, b = divmod(t, B)
+            back = psum.tile([P, 512], F32, name="acc", tag="acc", bufs=6)
+            for c in range(4):
+                cols = slice(c * P, (c + 1) * P)
+                nc.tensor.transpose(back[:, cols], turned_of[t][:, cols], ident[:])
             res_k = work.tile([P, NK], F32, name="res_k", tag="res_k", bufs=2)
-            nc.scalar.copy(out=res_k[:], in_=total[:])
+            nc.scalar.copy(out=res_k[:], in_=back[:])
             nc.scalar.dma_start(out=out_k[b, tt * P:(tt + 1) * P, :], in_=res_k[:])
 
         def finish(t, at):
@@ -276,6 +289,8 @@ def tile_selfattn_pa_kernel(tc, x, wq_words, wq_scales, wk_words, wk_scales, wv_
             at = new_at()
             q_bank(t, at, 0)
             q_bank(t, at, 1)
+            if t - 2 in TENSOR_ADDS:
+                tensor_add_second(t - 2)
             k_bank(t, at)
             if t == 2:
                 turn(2 * t + 2)
@@ -288,7 +303,9 @@ def tile_selfattn_pa_kernel(tc, x, wq_words, wq_scales, wk_words, wk_scales, wv_
                 v_bank(t + 2)
             finish(t, at)
             if t - 1 in TENSOR_ADDS:
-                tensor_add(t - 1)
+                tensor_add_first(t - 1)
+            if t == NTILES - 1:
+                tensor_add_second(t - 1)
             if t == 2:
                 prep_table(tab_q, 1)
                 spread_table(tab_q, tabx_q, 1, 0)

from contextlib import ExitStack

import concourse.mybir as mybir
from concourse.masks import make_identity

F32 = mybir.dt.float32
BF16 = mybir.dt.bfloat16
U8 = mybir.dt.uint8
U32 = mybir.dt.uint32
I32 = mybir.dt.int32
E5M2X4 = mybir.dt.float8_e5m2_x4
E2M1X4 = mybir.dt.float4_e2m1fn_x4
MULT = mybir.AluOpType.mult
ADD = mybir.AluOpType.add

B, T, D = 4, 512, 1024
NQ, NK = 1024, 512
P = 128
G = D // 512
TT = T // P
NTILES = B * TT
FLOPS = 2 * B * T * D * (NQ + 2 * NK)

XLOADS = [[0], [1]] + [[n, n + 1] for n in range(2, NTILES, 2)]
QGROUPS = [[0], [1], [2, 3], [4, 5, 6, 7], [8, 9, 10, 11], [12, 13, 14, 15]]
NR = NQ + NK
HOLDS = {2: 3, 6: 4, 10: 5}
HELD_BY = {3: 2, 4: 6, 5: 10}
TENSOR_ADDS = (5, 9, 13, 14)
WARM_FIRST, WARM_SECOND = 4, 2
SLOT = 4096 * 2


def tile_selfattn_pa_kernel(tc, x, wq_words, wq_scales, wk_words, wk_scales, wv_words, wv_scales,
                                        cos_q, sin_q, cos_k, sin_k, out_q, out_k, out_v):
    nc = tc.nc
    with ExitStack() as ctx:
        keep = ctx.enter_context(tc.tile_pool(name="keep", bufs=1))
        work = ctx.enter_context(tc.tile_pool(name="work", bufs=3))
        share = ctx.enter_context(tc.tile_pool(name="share", bufs=1))
        psum = ctx.enter_context(tc.psum_pool(name="psum", bufs=2))
        ctx.enter_context(tc.manual_schedule())

        planes = {}
        words = {}
        for key, width in (("q", NQ), ("k", NK), ("v", NK)):
            planes[key] = keep.tile([P, G, width], U8, name="plane_" + key, align_bytes=64)
            words[key] = keep.tile([P, G, 2 * width], U8, name="words_" + key, align_bytes=64)
            nc.vector.memset(planes[key][:].rearrange("p g n -> p (g n)").bitcast(I32), 0)
        warm = keep.tile([P, 2], F32, name="warm")
        nc.vector.memset(warm[:, 0:1], 0.0)
        nc.scalar.copy(out=warm[:, 1:2], in_=warm[:, 0:1])
        zeros = keep.tile([P, 512], BF16, name="zeros")
        nc.gpsimd.memset(zeros[:], 0.0)
        ident = keep.tile([P, P], F32, name="ident")
        make_identity(nc, ident[:])

        def idle_matmuls(n):
            for i in range(n):
                waste = psum.tile([P, 512], F32, name="acc", tag="acc", bufs=6)
                nc.tensor.matmul(out=waste[:], lhsT=zeros[:, 0:P], rhs=zeros[:], start=True, stop=True)

        x_of = {}
        x_sb = []
        for li, tiles in enumerate(XLOADS):
            x_sb.append(keep.tile([P, len(tiles), D], BF16, name="x%d" % li))
            for a, t in enumerate(tiles):
                x_of[t] = (li, a)
        tab_q = [keep.tile([P, 2, 2, NQ // 2], BF16, name="tabq%d" % tt) for tt in range(TT)]
        tab_k = [keep.tile([P, 2, 2, NK // 2], BF16, name="tabk%d" % tt) for tt in range(TT)]

        tabx_q = [None] + [keep.tile([P, 2, NQ], BF16, name="tabxq%d" % tt) for tt in range(1, TT)]
        tabx_k = [None] + [keep.tile([P, 2, NK], BF16, name="tabxk%d" % tt) for tt in range(1, TT)]

        def spread_table(tab, tabx, tt, w):
            nc.scalar.copy(out=tabx[tt][:, w, :].rearrange("p (i e) -> p i e", e=2),
                           in_=tab[tt][:, w, :, :].rearrange("p e i -> p i e"))

        def load_x(li):
            tiles = XLOADS[li]
            tt, b0 = divmod(tiles[0], B)
            nc.sync.dma_start(out=x_sb[li][:],
                              in_=x[b0:b0 + len(tiles), tt * P:(tt + 1) * P, :].rearrange("b p k -> p b k"))

        def load_weight(key, w_words, w_scales):
            for quad in range(4):
                nc.sync.dma_start(
                    out=planes[key][32 * quad:32 * quad + 4, :, :].bitcast(I32),
                    in_=w_scales[:, 4 * quad:4 * quad + 4, :].rearrange("g r n -> r g n").bitcast(I32))
            nc.sync.dma_start(out=words[key][:].bitcast(I32), in_=w_words.rearrange("g p n -> p g n").bitcast(I32))

        def load_table(tab, cos, sin, tt):
            nc.sync.dma_start(out=tab[tt][:, 0, 0, :], in_=cos[tt * P:(tt + 1) * P, :])
            nc.sync.dma_start(out=tab[tt][:, 1, 0, :], in_=sin[tt * P:(tt + 1) * P, :])

        def prep_table(tab, tt):
            nc.scalar.copy(out=tab[tt][:, 1, 1, :], in_=tab[tt][:, 0, 0, :])
            nc.scalar.mul(out=tab[tt][:, 0, 1, :], in_=tab[tt][:, 1, 0, :], mul=-1.0)

        load_x(0)
        load_x(1)
        load_weight("q", wq_words, wq_scales)
        load_table(tab_q, cos_q, sin_q, 0)
        load_weight("k", wk_words, wk_scales)
        load_table(tab_k, cos_k, sin_k, 0)
        load_x(2)
        load_weight("v", wv_words, wv_scales)
        for tt in range(1, TT):
            load_x(2 * tt + 1)
            load_x(2 * tt + 2)
            load_table(tab_q, cos_q, sin_q, tt)
            load_table(tab_k, cos_k, sin_k, tt)

        group_of = {}
        for qi, tiles in enumerate(QGROUPS):
            for a, t in enumerate(tiles):
                group_of[t] = (qi, a)
        grouped_of = {}
        codes_of = {}

        def turn(t):
            qi, a = group_of[t]
            if a == 0 and qi == 2:
                grouped_of[qi] = share.tile([P, 2048], BF16, name="pair", offset=0, align_bytes=64)
            elif a == 0 and qi in HELD_BY:
                grouped_of[qi] = share.tile([P, 4096], BF16, name="wide%d" % (qi % 2), offset=(qi % 2) * SLOT,
                                            align_bytes=64)
            elif a == 0:
                grouped_of[qi] = work.tile([P, len(QGROUPS[qi]) * 1024], BF16, name="grouped", tag="grouped",
                                           bufs=2, align_bytes=64)
            li, xa = x_of[t]
            xw = x_sb[li][:, xa, :].bitcast(F32)
            xt = psum.tile([P, 512], F32, name="xt", tag="xt", bufs=2)
            for g in range(G):
                for u in range(2):
                    s = 2 * g + u
                    nc.tensor.transpose(xt[:, s * P:(s + 1) * P], xw[:, 256 * g + u:256 * (g + 1):2], ident[:])
            nc.scalar.copy(
                out=grouped_of[qi][:, a * 1024:(a + 1) * 1024].bitcast(F32).rearrange("p (g r u) -> p g r u", g=G, u=2),
                in_=xt[:].rearrange("p (g u r) -> p g r u", g=G, u=2))

        def quantize(qi):
            n = len(QGROUPS[qi])
            codes = work.tile([P, n * 256], U32, name="codes", tag="codes", align_bytes=64)
            xs = work.tile([P, n * 256], U8, name="xs", tag="xs", align_bytes=64)
            nc.vector.quantize_mx(out=codes[:].bitcast(E5M2X4), scales=xs[:], in_=grouped_of[qi][:])
            codes_of[qi] = (codes, xs)

        def project(t, key, j):
            qi, a = group_of[t]
            codes, xs = codes_of[qi]
            acc = psum.tile([P, 512], F32, name="acc", tag="acc", bufs=6)
            for g in range(G):
                cols = slice(a * 256 + g * P, a * 256 + (g + 1) * P)
                nc.tensor.matmul_mx(out=acc[:], lhsT=codes[:, cols].bitcast(E5M2X4), lhsT_scale=xs[:, cols],
                                    rhs=words[key][:, g, 1024 * j:1024 * (j + 1)].bitcast(E2M1X4),
                                    rhs_scale=planes[key][:, g, 512 * j:512 * (j + 1)],
                                    start=(g == 0), stop=(g == G - 1))
            return acc

        def products(acc, at, bank, tab, tabx, j):
            if tabx is None:
                factors = tab[:, :, :, 256 * j:256 * (j + 1)].rearrange("p w e i -> p w i e")
            else:
                factors = tabx[:, :, 512 * j:512 * (j + 1)].rearrange("p w (i e) -> p w i e", e=2)
            nc.vector.tensor_tensor(
                out=at[:, bank, :, :].rearrange("p w (i e) -> p w i e", e=2),
                in0=acc[:].rearrange("p (i w) -> p w i", w=2).unsqueeze(3).to_broadcast([P, 2, 256, 2]),
                in1=factors,
                op=MULT)

        def new_at():
            return work.tile([P, 3, 2, 512], F32, name="at", tag="at", bufs=5)

        def q_bank(t, at, j):
            acc = project(t, "q", j)
            products(acc, at, j, tab_q[t // B], tabx_q[t // B], j)

        def k_bank(t, at):
            acc = project(t, "k", 0)
            products(acc, at, 2, tab_k[t // B], tabx_k[t // B], 0)

        def v_bank(t):
            tt, b = divmod(t, B)
            acc = project(t, "v", 0)
            res_v = work.tile([P, NK], F32, name="res_v", tag="res_v")
            nc.scalar.copy(out=res_v[:], in_=acc[:])
            nc.scalar.dma_start(out=out_v[b, tt * P:(tt + 1) * P, :], in_=res_v[:])

        def add_piece(adder, t, at, res, j):
            tt, b = divmod(t, B)
            rows = slice(tt * P, (tt + 1) * P)
            cols = slice(512 * j, 512 * (j + 1))
            adder.tensor_tensor(out=res[:, cols], in0=at[:, j, 0, :], in1=at[:, j, 1, :], op=ADD)
            if j < 2:
                nc.sync.dma_start(out=out_q[b, rows, cols], in_=res[:, cols])
            else:
                nc.sync.dma_start(out=out_k[b, rows, :], in_=res[:, cols])

        waiting = {}

        turned_of = {}

        def tensor_add_first(t):
            at = waiting[t]
            turned = psum.tile([P, 512], F32, name="acc", tag="acc", bufs=6)
            for c in range(4):
                cols = slice(c * P, (c + 1) * P)
                for w in range(2):
                    nc.tensor.matmul(out=turned[:, cols], lhsT=at[:, 2, w, cols], rhs=ident[:], is_transpose=True,
                                     start=(w == 0), stop=(w == 1))
            turned_of[t] = work.tile([P, NK], F32, name="turned", tag="turned", bufs=2)
            nc.scalar.copy(out=turned_of[t][:], in_=turned[:])

        def tensor_add_second(t):
            tt, b = divmod(t, B)
            back = psum.tile([P, 512], F32, name="acc", tag="acc", bufs=6)
            for c in range(4):
                cols = slice(c * P, (c + 1) * P)
                nc.tensor.transpose(back[:, cols], turned_of[t][:, cols], ident[:])
            res_k = work.tile([P, NK], F32, name="res_k", tag="res_k", bufs=2)
            nc.scalar.copy(out=res_k[:], in_=back[:])
            nc.scalar.dma_start(out=out_k[b, tt * P:(tt + 1) * P, :], in_=res_k[:])

        def finish(t, at):
            tt, b = divmod(t, B)
            rows = slice(tt * P, (tt + 1) * P)
            if t in HOLDS:
                res = share.tile([P, NR], F32, name="held%d" % (HOLDS[t] % 2), offset=(HOLDS[t] % 2) * SLOT,
                                 align_bytes=64)
            else:
                res = work.tile([P, NR], F32, name="res", tag="res", bufs=4)
            if t in TENSOR_ADDS and t < NTILES - 2:
                nc.gpsimd.tensor_tensor(out=res[:, 0:NQ].rearrange("p (j c) -> p j c", j=2),
                                        in0=at[:, 0:2, 0, :], in1=at[:, 0:2, 1, :], op=ADD)
                nc.sync.dma_start(out=out_q[b, rows, :], in_=res[:, 0:NQ])
                waiting[t] = at
            elif t < NTILES - 2:
                nc.gpsimd.tensor_tensor(out=res[:].rearrange("p (j c) -> p j c", j=3),
                                        in0=at[:, :, 0, :], in1=at[:, :, 1, :], op=ADD)
                nc.sync.dma_start(out=out_q[b, rows, :], in_=res[:, 0:NQ])
                nc.sync.dma_start(out=out_k[b, rows, :], in_=res[:, NQ:NR])
            elif t == NTILES - 2:
                add_piece(nc.gpsimd, t, at, res, 0)
                add_piece(nc.gpsimd, t, at, res, 1)
                waiting[t] = at
            else:
                add_piece(nc.gpsimd, t, at, res, 0)
                add_piece(nc.vector, t, at, res, 1)
                add_piece(nc.vector, t, at, res, 2)

        idle_matmuls(WARM_FIRST)
        turn(0)
        quantize(0)
        turn(1)
        quantize(1)
        idle_matmuls(WARM_SECOND)
        nc.vector.tensor_copy(out=tab_q[0][:, 1, 1, :], in_=tab_q[0][:, 0, 0, :])
        nc.vector.tensor_scalar_mul(out=tab_q[0][:, 0, 1, :], in0=tab_q[0][:, 1, 0, :], scalar1=-1.0)
        prep_table(tab_k, 0)

        at_0 = new_at()
        at_1 = new_at()
        q_bank(0, at_0, 0)
        q_bank(0, at_0, 1)
        k_bank(0, at_0)
        res_0 = work.tile([P, NR], F32, name="res", tag="res", bufs=4)
        nc.gpsimd.tensor_tensor(out=res_0[:, 0:NQ].rearrange("p (j c) -> p j c", j=2),
                                in0=at_0[:, 0:2, 0, :], in1=at_0[:, 0:2, 1, :], op=ADD)
        nc.sync.dma_start(out=out_q[0, 0:P, :], in_=res_0[:, 0:NQ])
        q_bank(1, at_1, 0)
        q_bank(1, at_1, 1)
        turn(2)
        turn(3)
        quantize(2)
        held_k = share.tile([P, NK], F32, name="held_k", offset=0, align_bytes=64)
        nc.gpsimd.tensor_tensor(out=held_k[:], in0=at_0[:, 2, 0, :], in1=at_0[:, 2, 1, :], op=ADD)
        nc.sync.dma_start(out=out_k[0, 0:P, :], in_=held_k[:])
        k_bank(1, at_1)
        v_bank(0)
        turn(4)
        turn(5)
        v_bank(1)
        finish(1, at_1)

        for t in range(2, NTILES):
            tt, b = divmod(t, B)
            more = tt + 1 < TT
            at = new_at()
            q_bank(t, at, 0)
            q_bank(t, at, 1)
            if t - 2 in TENSOR_ADDS:
                tensor_add_second(t - 2)
            k_bank(t, at)
            if t == 2:
                turn(2 * t + 2)
                turn(2 * t + 3)
            if t in HOLDS:
                quantize(HOLDS[t])
            if t < NTILES - 2:
                v_bank(t)
            if t in (NTILES - 4, NTILES - 3):
                v_bank(t + 2)
            finish(t, at)
            if t - 1 in TENSOR_ADDS:
                tensor_add_first(t - 1)
            if t == NTILES - 1:
                tensor_add_second(t - 1)
            if t == 2:
                prep_table(tab_q, 1)
                spread_table(tab_q, tabx_q, 1, 0)
                spread_table(tab_q, tabx_q, 1, 1)
                prep_table(tab_k, 1)
                spread_table(tab_k, tabx_k, 1, 0)
                spread_table(tab_k, tabx_k, 1, 1)
            inner = more and tt > 0
            if inner and b in (0, 1):
                turn(4 * tt + 4 + 2 * b)
                turn(4 * tt + 5 + 2 * b)
            if inner and b == 1:
                prep_table(tab_q, tt + 1)
                prep_table(tab_k, tt + 1)
                spread_table(tab_q, tabx_q, tt + 1, 0)
            if inner and b == 2:
                spread_table(tab_q, tabx_q, tt + 1, 1)
                spread_table(tab_k, tabx_k, tt + 1, 0)
                spread_table(tab_k, tabx_k, tt + 1, 1)
